import numpy as np
import ml_dtypes


def mxq(x, axis, fmt="e4m3"):
    dtype, down = {"e4m3": (ml_dtypes.float8_e4m3fn, 7), "e5m2": (ml_dtypes.float8_e5m2, 14)}[fmt]
    v = np.moveaxis(np.asarray(x, np.float32).astype(ml_dtypes.bfloat16).astype(np.float64), axis, -1)
    blocks = v.reshape(v.shape[:-1] + (-1, 32))
    amax = np.abs(blocks).max(-1, keepdims=True)
    byte = np.maximum(np.where(amax > 0, np.frexp(amax)[1] - 1 + 127, 0) - down, 1)
    scale = np.exp2(byte - 127.0)
    codes = (blocks / scale).astype(np.float32).astype(dtype).astype(np.float64)
    return np.moveaxis((codes * scale).reshape(v.shape), -1, axis)


WIDE = False


def mx_kscale(k):
    if not WIDE:
        return np.ones(k)
    levels = np.array([10, -10, 5, -5, 0])
    a = np.random.permutation(np.resize(levels, k // 512 * 4)).reshape(k // 512, 4)
    idx = np.arange(k)
    return np.exp2(a[idx // 512, idx % 128 // 32])


BF16 = ml_dtypes.bfloat16


def bf(x):
    return np.asarray(x, np.float32).astype(BF16)


def f64(x):
    return np.asarray(x).astype(np.float64)


N, I, O = 8192, 1024, 128


def sigmoid(v):
    return 1.0 / (1.0 + np.exp(-v))


def setup_inputs():
    t = np.exp2(np.round(np.log2(mx_kscale(I)) / 2))
    u = t / t.min()
    x = np.random.standard_normal((N, I)) * 1.5 / np.sqrt(I) * u
    p = sigmoid(np.random.standard_normal((O, I)) * 1.5) / (u * u)
    mag_logits = np.log(p / (1.0 - p))
    sgn_logits = np.random.standard_normal((O, I)) * 1.5
    return {"x": bf(x),
            "weight_logits": bf(np.stack([mag_logits, sgn_logits], axis=-1)),
            "scale": bf(1.0 + 0.1 * np.random.standard_normal(O)),
            "shift": bf(0.1 * np.random.standard_normal(O)),
            "noise": bf(np.random.standard_normal((N, O)))}


def reference(x, weight_logits, scale, shift, noise):
    xf = f64(x)
    weight_p = sigmoid(f64(weight_logits))
    p_mag = weight_p[..., 0]
    p_sgn = weight_p[..., 1]
    s = 2.0 * p_sgn - 1.0
    weight_mean = p_mag * s
    weight_var = p_mag - (p_mag * p_mag) * (s * s)
    out_mean = mxq(xf, 1, "e4m3") @ mxq(weight_mean, 1, "e4m3").T
    out_var = mxq(xf * xf, 1, "e4m3") @ mxq(weight_var, 1, "e4m3").T
    out = out_mean + np.sqrt(out_var) * f64(noise)
    out = out * f64(scale)[None, :] + f64(shift)[None, :]
    return out

@@ -1,0 +1,165 @@
+from contextlib import ExitStack
+
+import concourse.mybir as mybir
+from concourse.masks import make_identity
+
+FP8X4 = mybir.dt.float8_e4m3fn_x4
+BF16 = mybir.dt.bfloat16
+F32 = mybir.dt.float32
+U32 = mybir.dt.uint32
+U8 = mybir.dt.uint8
+ACT = mybir.ActivationFunctionType
+ALU = mybir.AluOpType
+
+N_TOK, K_IN, N_OUT = 8192, 1024, 128
+FLOPS = 2 * 2 * N_TOK * K_IN * N_OUT
+P = 128
+T = N_TOK // P
+CH = 4
+NCH = T // CH
+
+
+def tile_ternarylinear_t_kernel(tc, x, weight_logits, scale, shift, noise, out):
+    nc = tc.nc
+    x_v = x.rearrange("(p t) k -> p (t k)", t=T)
+    noise_v = noise.rearrange("(p t) o -> p (t o)", t=T)
+    out_v = out.rearrange("(p t) o -> p (t o)", t=T)
+
+    with ExitStack() as ctx:
+        const = ctx.enter_context(tc.tile_pool(name="const", bufs=1))
+        xpool = ctx.enter_context(tc.tile_pool(name="xpool", bufs=4))
+        gpool = ctx.enter_context(tc.tile_pool(name="gpool", bufs=3))
+        cpool = ctx.enter_context(tc.tile_pool(name="cpool", bufs=3))
+        epool = ctx.enter_context(tc.tile_pool(name="epool", bufs=3))
+        psx = ctx.enter_context(tc.psum_pool(name="psx", bufs=4))
+        psa = ctx.enter_context(tc.psum_pool(name="psa", bufs=2))
+
+        logit = const.tile([P, 2 * K_IN], BF16)
+        nc.sync.dma_start(out=logit[:], in_=weight_logits.rearrange("o i c -> o (i c)"))
+        scale_b = const.tile([P, N_OUT], BF16)
+        nc.scalar.dma_start(out=scale_b[:], in_=scale.partition_broadcast(P))
+        shift_b = const.tile([P, N_OUT], BF16)
+        nc.scalar.dma_start(out=shift_b[:], in_=shift.partition_broadcast(P))
+        noise_sb = const.tile([P, T * N_OUT], BF16)
+
+        ident_f = const.tile([P, P], F32)
+        make_identity(nc, ident_f[:])
+        ident_b = const.tile([P, P], BF16)
+        make_identity(nc, ident_b[:])
+
+        lv = logit[:].rearrange("o (j e c) -> o c e j", e=2, c=2)
+        p_mag = const.tile([P, 2, 512], F32)
+        nc.scalar.activation(out=p_mag[:], in_=lv[:, 0], func=ACT.Sigmoid)
+        sgn = const.tile([P, 2, 512], F32)
+        nc.scalar.activation(out=sgn[:], in_=lv[:, 1], func=ACT.Tanh, scale=0.5)
+        sgn2 = const.tile([P, 2, 512], F32)
+        nc.scalar.activation(out=sgn2[:], in_=sgn[:], func=ACT.Square)
+        w_bf = const.tile([P, 2, 2, 512], BF16)
+        nc.vector.tensor_tensor(out=w_bf[:, 0], in0=p_mag[:], in1=sgn[:], op=ALU.mult)
+        rest = const.tile([P, 2, 512], F32)
+        nc.vector.tensor_tensor(out=rest[:], in0=p_mag[:], in1=sgn2[:], op=ALU.mult)
+        nc.vector.tensor_scalar(out=rest[:], in0=rest[:], scalar1=-1.0, scalar2=1.0, op0=ALU.mult, op1=ALU.add)
+        nc.vector.tensor_tensor(out=w_bf[:, 1], in0=p_mag[:], in1=rest[:], op=ALU.mult)
+
+        w_grp = const.tile([P, 2, 2, N_OUT, 4], BF16, align_bytes=64)
+        for which in range(2):
+            wt = psx.tile([P, 8, P], BF16, tag="xt")
+            for m in range(4):
+                for e in range(2):
+                    nc.tensor.transpose(wt[:, 2 * m + e, :], w_bf[:, which, e, P * m : P * (m + 1)], ident_b[:])
+            nc.vector.tensor_copy(out=w_grp[:, which], in_=wt[:].rearrange("p (g t) o -> p g o t", t=4))
+        w_codes = const.tile([P, 4 * N_OUT], U32, align_bytes=64)
+        w_scales = const.tile([P, 4 * N_OUT], U8, align_bytes=64)
+        nc.vector.quantize_mx(
+            out=w_codes[:].bitcast(FP8X4),
+            scales=w_scales[:],
+            in_=w_grp[:].rearrange("p w g o t -> p (w g o t)"),
+        )
+
+        state = {}
+
+        def load(c):
+            xt = xpool.tile([P, CH * K_IN], BF16, tag="x")
+            nc.sync.dma_start(out=xt[:], in_=x_v[:, CH * K_IN * c : CH * K_IN * (c + 1)])
+            state[("x", c)] = xt
+            if c % 4 == 0:
+                q = c // 4
+                w = T * N_OUT // 4
+                nc.sync.dma_start(out=noise_sb[:, w * q : w * (q + 1)], in_=noise_v[:, w * q : w * (q + 1)])
+
+        def front(c):
+            xt = state[("x", c)]
+            xw = xt[:].bitcast(F32)
+            gx = gpool.tile([P, 4096], BF16, tag="gx", align_bytes=64)
+            gs = gpool.tile([P, 4096], BF16, tag="gs", align_bytes=64)
+            gxw = gx[:].bitcast(F32)
+            n_s = 2 + c % 2
+            for b in range(4):
+                g, h = divmod(b, 2)
+                bank = psx.tile([P, 512], F32, tag="xt")
+                for u in range(2):
+                    for j2 in range(2):
+                        col = 512 * (2 * h + j2) + 256 * g + 128 * u
+                        nc.tensor.transpose(bank[:, P * (2 * u + j2) : P * (2 * u + j2 + 1)], xw[:, col : col + P], ident_f[:])
+                nc.scalar.copy(
+                    out=gxw[:, 512 * b : 512 * (b + 1)].rearrange("p (t u) -> p t u", u=2),
+                    in_=bank[:].rearrange("p (u t) -> p t u", u=2),
+                )
+                if b < n_s:
+                    nc.scalar.activation(
+                        out=gs[:, 1024 * b : 1024 * (b + 1)].rearrange("p (t u e) -> p t u e", u=2, e=2),
+                        in_=bank[:].bitcast(BF16).rearrange("p (u t e) -> p t u e", u=2, e=2),
+                        func=ACT.Square,
+                    )
+            nc.vector.tensor_tensor(out=gs[:, 1024 * n_s :], in0=gx[:, 1024 * n_s :], in1=gx[:, 1024 * n_s :], op=ALU.mult)
+            state[("g", c)] = (gx, gs)
+
+        def quant_mx(c):
+            gx, gs = state[("g", c)]
+            ops = []
+            for name, src in (("x", gx), ("s", gs)):
+                codes = cpool.tile([P, 1024], U32, tag="c" + name, name="codes_" + name, align_bytes=64)
+                scl = cpool.tile([P, 1024], U8, tag="p" + name, name="scl_" + name, align_bytes=64)
+                nc.vector.quantize_mx(out=codes[:].bitcast(FP8X4), scales=scl[:], in_=src[:])
+                ops.append((codes, scl))
+            accs = []
+            for which in range(2):
+                codes, scl = ops[which]
+                acc = psa.tile([P, 512], F32, tag="acc%d" % which, name="acc%d" % which)
+                for j in range(CH):
+                    for g in range(2):
+                        a0 = 512 * g + P * j
+                        w0 = P * (2 * which + g)
+                        nc.tensor.matmul_mx(
+                            out=acc[:, P * j : P * (j + 1)],
+                            lhsT=codes[:, a0 : a0 + P].bitcast(FP8X4),
+                            lhsT_scale=scl[:, a0 : a0 + P],
+                            rhs=w_codes[:, w0 : w0 + P].bitcast(FP8X4),
+                            rhs_scale=w_scales[:, w0 : w0 + P],
+                            start=(g == 0),
+                            stop=(g == 1),
+                        )
+                accs.append(acc)
+            state[("a", c)] = accs
+
+        def epilogue(c):
+            mean, var = state[("a", c)]
+            w = CH * N_OUT
+            sd = epool.tile([P, w], F32, tag="sd")
+            nc.scalar.activation(out=sd[:], in_=var[:], func=ACT.Sqrt)
+            ot = epool.tile([P, w], F32, tag="ot")
+            nc.vector.tensor_tensor(out=ot[:], in0=sd[:], in1=noise_sb[:, w * c : w * (c + 1)], op=ALU.mult)
+            nc.vector.tensor_tensor(out=ot[:], in0=ot[:], in1=mean[:], op=ALU.add)
+            o3 = ot[:].rearrange("p (t o) -> p t o", t=CH)
+            nc.vector.tensor_tensor(out=o3, in0=o3, in1=scale_b[:].unsqueeze(1).to_broadcast([P, CH, N_OUT]), op=ALU.mult)
+            nc.vector.tensor_tensor(out=o3, in0=o3, in1=shift_b[:].unsqueeze(1).to_broadcast([P, CH, N_OUT]), op=ALU.add)
+            nc.sync.dma_start(out=out_v[:, w * c : w * (c + 1)], in_=ot[:])
+
+        for c in range(NCH + 2):
+            if c < NCH:
+                load(c)
+                front(c)
+            if 1 <= c <= NCH:
+                quant_mx(c - 1)
+            if c >= 2:
+                epilogue(c - 2)

@@ -17,6 +17,7 @@ P = 128
 T = N_TOK // P
 CH = 4
 NCH = T // CH
+W = CH * P
 
 
 def tile_ternarylinear_t_kernel(tc, x, weight_logits, scale, shift, noise, out):
@@ -32,16 +33,136 @@ def tile_ternarylinear_t_kernel(tc, x, weight_logits, scale, shift, noise, out):
         cpool = ctx.enter_context(tc.tile_pool(name="cpool", bufs=3))
         epool = ctx.enter_context(tc.tile_pool(name="epool", bufs=3))
         psx = ctx.enter_context(tc.psum_pool(name="psx", bufs=4))
-        psa = ctx.enter_context(tc.psum_pool(name="psa", bufs=2))
+        psa = ctx.enter_context(tc.psum_pool(name="psa", bufs=1))
+        ctx.enter_context(tc.manual_schedule())
+
+        state = {}
+
+        def load(c):
+            xt = xpool.tile([P, CH * K_IN], BF16, tag="x", name="xt")
+            nc.sync.dma_start(out=xt[:], in_=x_v[:, CH * K_IN * c : CH * K_IN * (c + 1)])
+            state[("x", c)] = xt
+
+        def load_noise(q):
+            w = T * N_OUT // 4
+            nc.sync.dma_start(out=noise_sb[:, w * q : w * (q + 1)], in_=noise_v[:, w * q : w * (q + 1)])
+
+        def x_transposes(c, b):
+            xw = state[("x", c)][:].bitcast(F32)
+            g, h = divmod(b, 2)
+            bank = psx.tile([P, 512], F32, tag="xt", name="bank")
+            for u in range(2):
+                for j2 in range(2):
+                    col = 512 * (2 * h + j2) + 256 * g + 128 * u
+                    nc.tensor.transpose(bank[:, P * (2 * u + j2) : P * (2 * u + j2 + 1)], xw[:, col : col + P], ident_f[:])
+            state[("b", c, b)] = bank
+
+        def front_bank(c, b):
+            if b == 0:
+                gx_new = gpool.tile([P, 4096], BF16, tag="gx", name="gx", align_bytes=64)
+                gs_new = gpool.tile([P, 4096], BF16, tag="gs", name="gs", align_bytes=64)
+                state[("g", c)] = (gx_new, gs_new)
+            gx, gs = state[("g", c)]
+            bank = state[("b", c, b)]
+            nc.scalar.copy(
+                out=gx[:].bitcast(F32)[:, 512 * b : 512 * (b + 1)].rearrange("p (t u) -> p t u", u=2),
+                in_=bank[:].rearrange("p (u t) -> p t u", u=2),
+            )
+            if b < 2:
+                nc.scalar.activation(
+                    out=gs[:, 1024 * b : 1024 * (b + 1)].rearrange("p (t u e) -> p t u e", u=2, e=2),
+                    in_=bank[:].bitcast(BF16).rearrange("p (u t e) -> p t u e", u=2, e=2),
+                    func=ACT.Square,
+                )
+
+        def quantise(c):
+            gx, gs = state[("g", c)]
+            nc.vector.tensor_tensor(out=gs[:, 2048:], in0=gx[:, 2048:], in1=gx[:, 2048:], op=ALU.mult)
+            ops = []
+            for nm, src in (("x", gx), ("s", gs)):
+                codes = cpool.tile([P, 1024], U32, tag="c" + nm, name="codes_" + nm, align_bytes=64)
+                scl = cpool.tile([P, 1024], U8, tag="p" + nm, name="scl_" + nm, align_bytes=64)
+                nc.vector.quantize_mx(out=codes[:].bitcast(FP8X4), scales=scl[:], in_=src[:])
+                ops.append((codes, scl))
+            state[("q", c)] = ops
+
+        def mx(c):
+            ops = state[("q", c)]
+            accs = {}
+            for which in (1, 0):
+                codes, scl = ops[which]
+                acc = psa.tile([P, W], F32, tag="acc%d" % which, name="acc%d" % which)
+                for g in range(2):
+                    w0 = P * (2 * which + g)
+                    nc.tensor.matmul_mx(
+                        out=acc[:],
+                        lhsT=w_codes[:, w0 : w0 + P].bitcast(FP8X4),
+                        lhsT_scale=w_scales[:, w0 : w0 + P],
+                        rhs=codes[:, W * g : W * (g + 1)].bitcast(FP8X4),
+                        rhs_scale=scl[:, W * g : W * (g + 1)],
+                        start=(g == 0),
+                        stop=(g == 1),
+                    )
+                accs[which] = acc
+            state[("a", c)] = accs
+
+        def noise_transposes(c):
+            nt = psa.tile([P, W], BF16, tag="nt", name="nt")
+            for j in range(CH):
+                col = N_OUT * (CH * c + j)
+                nc.tensor.transpose(nt[:, P * j : P * (j + 1)], noise_sb[:, col : col + N_OUT], ident_b[:])
+            state[("n", c)] = nt
+
+        def root(c):
+            sd = epool.tile([P, W], F32, tag="sd", name="sd")
+            nc.scalar.activation(out=sd[:], in_=state[("a", c)][1][:], func=ACT.Sqrt)
+            state[("sd", c)] = sd
+
+        def noise_term(c):
+            tt = epool.tile([P, W], F32, tag="tt", name="tt")
+            nc.vector.scalar_tensor_tensor(
+                out=tt[:], in0=state[("sd", c)][:], scalar=per_out[:, 0:1], in1=state[("n", c)][:], op0=ALU.mult, op1=ALU.mult
+            )
+            state[("t", c)] = tt
+
+        def add_mean(c):
+            z = epool.tile([P, W], F32, tag="z", name="z")
+            nc.vector.scalar_tensor_tensor(
+                out=z[:], in0=state[("a", c)][0][:], scalar=per_out[:, 0:1], in1=state[("t", c)][:], op0=ALU.mult, op1=ALU.add
+            )
+            state[("z", c)] = z
+
+        def z_transposes(c):
+            z = state[("z", c)]
+            zt = psa.tile([P, W], F32, tag="zt", name="zt")
+            for j in range(CH):
+                nc.tensor.transpose(zt[:, P * j : P * (j + 1)], z[:, P * j : P * (j + 1)], ident_f[:])
+            state[("zt", c)] = zt
+
+        def finish(c):
+            ot = epool.tile([P, CH, N_OUT], F32, tag="ot", name="ot")
+            nc.vector.tensor_tensor(
+                out=ot[:],
+                in0=state[("zt", c)][:].rearrange("p (t o) -> p t o", t=CH),
+                in1=shift_b[:].unsqueeze(1).to_broadcast([P, CH, N_OUT]),
+                op=ALU.add,
+            )
+            nc.sync.dma_start(out=out_v[:, W * c : W * (c + 1)], in_=ot[:].rearrange("p t o -> p (t o)"))
 
         logit = const.tile([P, 2 * K_IN], BF16)
         nc.sync.dma_start(out=logit[:], in_=weight_logits.rearrange("o i c -> o (i c)"))
-        scale_b = const.tile([P, N_OUT], BF16)
-        nc.scalar.dma_start(out=scale_b[:], in_=scale.partition_broadcast(P))
+        noise_sb = const.tile([P, T * N_OUT], BF16)
+        load(0)
+        load(1)
+        load_noise(0)
+        load(2)
+        load(3)
+
+        rows = const.tile([P, P], BF16)
+        nc.gpsimd.memset(rows[:], 0.0)
+        nc.scalar.dma_start(out=rows[0:1, :], in_=scale.rearrange("(a o) -> a o", a=1))
         shift_b = const.tile([P, N_OUT], BF16)
         nc.scalar.dma_start(out=shift_b[:], in_=shift.partition_broadcast(P))
-        noise_sb = const.tile([P, T * N_OUT], BF16)
-
         ident_f = const.tile([P, P], F32)
         make_identity(nc, ident_f[:])
         ident_b = const.tile([P, P], BF16)
@@ -60,106 +181,65 @@ def tile_ternarylinear_t_kernel(tc, x, weight_logits, scale, shift, noise, out):
         nc.vector.tensor_tensor(out=rest[:], in0=p_mag[:], in1=sgn2[:], op=ALU.mult)
         nc.vector.tensor_scalar(out=rest[:], in0=rest[:], scalar1=-1.0, scalar2=1.0, op0=ALU.mult, op1=ALU.add)
         nc.vector.tensor_tensor(out=w_bf[:, 1], in0=p_mag[:], in1=rest[:], op=ALU.mult)
-
         w_grp = const.tile([P, 2, 2, N_OUT, 4], BF16, align_bytes=64)
-        for which in range(2):
-            wt = psx.tile([P, 8, P], BF16, tag="xt")
-            for m in range(4):
-                for e in range(2):
-                    nc.tensor.transpose(wt[:, 2 * m + e, :], w_bf[:, which, e, P * m : P * (m + 1)], ident_b[:])
-            nc.vector.tensor_copy(out=w_grp[:, which], in_=wt[:].rearrange("p (g t) o -> p g o t", t=4))
         w_codes = const.tile([P, 4 * N_OUT], U32, align_bytes=64)
         w_scales = const.tile([P, 4 * N_OUT], U8, align_bytes=64)
-        nc.vector.quantize_mx(
-            out=w_codes[:].bitcast(FP8X4),
-            scales=w_scales[:],
-            in_=w_grp[:].rearrange("p w g o t -> p (w g o t)"),
-        )
+        per_out = const.tile([P, 1], F32)
 
-        state = {}
-
-        def load(c):
-            xt = xpool.tile([P, CH * K_IN], BF16, tag="x")
-            nc.sync.dma_start(out=xt[:], in_=x_v[:, CH * K_IN * c : CH * K_IN * (c + 1)])
-            state[("x", c)] = xt
-            if c % 4 == 0:
-                q = c // 4
-                w = T * N_OUT // 4
-                nc.sync.dma_start(out=noise_sb[:, w * q : w * (q + 1)], in_=noise_v[:, w * q : w * (q + 1)])
-
-        def front(c):
-            xt = state[("x", c)]
-            xw = xt[:].bitcast(F32)
-            gx = gpool.tile([P, 4096], BF16, tag="gx", align_bytes=64)
-            gs = gpool.tile([P, 4096], BF16, tag="gs", align_bytes=64)
-            gxw = gx[:].bitcast(F32)
-            n_s = 2 + c % 2
-            for b in range(4):
-                g, h = divmod(b, 2)
-                bank = psx.tile([P, 512], F32, tag="xt")
-                for u in range(2):
-                    for j2 in range(2):
-                        col = 512 * (2 * h + j2) + 256 * g + 128 * u
-                        nc.tensor.transpose(bank[:, P * (2 * u + j2) : P * (2 * u + j2 + 1)], xw[:, col : col + P], ident_f[:])
-                nc.scalar.copy(
-                    out=gxw[:, 512 * b : 512 * (b + 1)].rearrange("p (t u) -> p t u", u=2),
-                    in_=bank[:].rearrange("p (u t) -> p t u", u=2),
-                )
-                if b < n_s:
-                    nc.scalar.activation(
-                        out=gs[:, 1024 * b : 1024 * (b + 1)].rearrange("p (t u e) -> p t u e", u=2, e=2),
-                        in_=bank[:].bitcast(BF16).rearrange("p (u t e) -> p t u e", u=2, e=2),
-                        func=ACT.Square,
-                    )
-            nc.vector.tensor_tensor(out=gs[:, 1024 * n_s :], in0=gx[:, 1024 * n_s :], in1=gx[:, 1024 * n_s :], op=ALU.mult)
-            state[("g", c)] = (gx, gs)
-
-        def quant_mx(c):
-            gx, gs = state[("g", c)]
-            ops = []
-            for name, src in (("x", gx), ("s", gs)):
-                codes = cpool.tile([P, 1024], U32, tag="c" + name, name="codes_" + name, align_bytes=64)
-                scl = cpool.tile([P, 1024], U8, tag="p" + name, name="scl_" + name, align_bytes=64)
-                nc.vector.quantize_mx(out=codes[:].bitcast(FP8X4), scales=scl[:], in_=src[:])
-                ops.append((codes, scl))
-            accs = []
+        def weight_transposes():
             for which in range(2):
-                codes, scl = ops[which]
-                acc = psa.tile([P, 512], F32, tag="acc%d" % which, name="acc%d" % which)
-                for j in range(CH):
-                    for g in range(2):
-                        a0 = 512 * g + P * j
-                        w0 = P * (2 * which + g)
-                        nc.tensor.matmul_mx(
-                            out=acc[:, P * j : P * (j + 1)],
-                            lhsT=codes[:, a0 : a0 + P].bitcast(FP8X4),
-                            lhsT_scale=scl[:, a0 : a0 + P],
-                            rhs=w_codes[:, w0 : w0 + P].bitcast(FP8X4),
-                            rhs_scale=w_scales[:, w0 : w0 + P],
-                            start=(g == 0),
-                            stop=(g == 1),
-                        )
-                accs.append(acc)
-            state[("a", c)] = accs
+                wt = psa.tile([P, 8, P], BF16, tag="acc%d" % which, name="wt%d" % which)
+                for m in range(4):
+                    for e in range(2):
+                        nc.tensor.transpose(wt[:, 2 * m + e, :], w_bf[:, which, e, P * m : P * (m + 1)], ident_b[:])
+                state[("wt", which)] = wt
+            rt = psa.tile([P, P], BF16, tag="nt", name="rt")
+            nc.tensor.transpose(rt[:], rows[:], ident_b[:])
+            state["rt"] = rt
 
-        def epilogue(c):
-            mean, var = state[("a", c)]
-            w = CH * N_OUT
-            sd = epool.tile([P, w], F32, tag="sd")
-            nc.scalar.activation(out=sd[:], in_=var[:], func=ACT.Sqrt)
-            ot = epool.tile([P, w], F32, tag="ot")
-            nc.vector.tensor_tensor(out=ot[:], in0=sd[:], in1=noise_sb[:, w * c : w * (c + 1)], op=ALU.mult)
-            nc.vector.tensor_tensor(out=ot[:], in0=ot[:], in1=mean[:], op=ALU.add)
-            o3 = ot[:].rearrange("p (t o) -> p t o", t=CH)
-            nc.vector.tensor_tensor(out=o3, in0=o3, in1=scale_b[:].unsqueeze(1).to_broadcast([P, CH, N_OUT]), op=ALU.mult)
-            nc.vector.tensor_tensor(out=o3, in0=o3, in1=shift_b[:].unsqueeze(1).to_broadcast([P, CH, N_OUT]), op=ALU.add)
-            nc.sync.dma_start(out=out_v[:, w * c : w * (c + 1)], in_=ot[:])
+        def weight_quantise():
+            for which in range(2):
+                nc.vector.tensor_copy(out=w_grp[:, which], in_=state[("wt", which)][:].rearrange("p (g t) o -> p g o t", t=4))
+            nc.vector.tensor_copy(out=per_out[:], in_=state["rt"][:, 0:1])
+            nc.vector.quantize_mx(
+                out=w_codes[:].bitcast(FP8X4),
+                scales=w_scales[:],
+                in_=w_grp[:].rearrange("p w g o t -> p (w g o t)"),
+            )
 
-        for c in range(NCH + 2):
-            if c < NCH:
-                load(c)
-                front(c)
-            if 1 <= c <= NCH:
-                quant_mx(c - 1)
-            if c >= 2:
-                epilogue(c - 2)
+        for b in range(4):
+            x_transposes(0, b)
+
+        def live(c):
+            return 0 <= c < NCH
+
+        for s in range(NCH + 3):
+            if live(s + 4):
+                load(s + 4)
+            if s in (2, 6, 10):
+                load_noise((s + 2) // 4)
+            if live(s - 2):
+                mx(s - 2)
+            if live(s - 3):
+                z_transposes(s - 3)
+            if live(s - 2):
+                noise_transposes(s - 2)
+            for b in range(4):
+                if live(s):
+                    front_bank(s, b)
+                if live(s + 1):
+                    x_transposes(s + 1, b)
+                if b == 1 and live(s - 2):
+                    root(s - 2)
+                if b == 1 and s == 0:
+                    weight_transposes()
+            if s == 0:
+                weight_quantise()
+            if live(s - 1):
+                quantise(s - 1)
+            if live(s - 2):
+                noise_term(s - 2)
+            if live(s - 3):
+                finish(s - 3)
+            if live(s - 2):
+                add_mean(s - 2)

@@ -15,9 +15,11 @@ N_TOK, K_IN, N_OUT = 8192, 1024, 128
 FLOPS = 2 * 2 * N_TOK * K_IN * N_OUT
 P = 128
 T = N_TOK // P
-CH = 4
-NCH = T // CH
-W = CH * P
+LD = 4
+SIZES = [4, 4, 4, 4, 4, 4, 4, 4, 4, 4, 4, 4, 4, 4, 4, 2, 2]
+STARTS = [0, 4, 8, 12, 16, 20, 24, 28, 32, 36, 40, 44, 48, 52, 56, 60, 62]
+NCH = len(SIZES)
+S_SQ = [0, 0, 1, 0, 1, 0, 1, 0, 1, 0, 1, 1, 1, 1, 2, 1, 1]
 
 
 def tile_ternarylinear_t_kernel(tc, x, weight_logits, scale, shift, noise, out):
@@ -38,22 +40,23 @@ def tile_ternarylinear_t_kernel(tc, x, weight_logits, scale, shift, noise, out):
 
         state = {}
 
-        def load(c):
-            xt = xpool.tile([P, CH * K_IN], BF16, tag="x", name="xt")
-            nc.sync.dma_start(out=xt[:], in_=x_v[:, CH * K_IN * c : CH * K_IN * (c + 1)])
-            state[("x", c)] = xt
+        def load(q):
+            xt = xpool.tile([P, LD * K_IN], BF16, tag="x", name="xt")
+            nc.sync.dma_start(out=xt[:], in_=x_v[:, LD * K_IN * q : LD * K_IN * (q + 1)])
+            state[("x", q)] = xt
 
         def load_noise(q):
             w = T * N_OUT // 4
             nc.sync.dma_start(out=noise_sb[:, w * q : w * (q + 1)], in_=noise_v[:, w * q : w * (q + 1)])
 
         def x_transposes(c, b):
-            xw = state[("x", c)][:].bitcast(F32)
-            g, h = divmod(b, 2)
+            t0, nj = STARTS[c], SIZES[c]
+            xw = state[("x", t0 // LD)][:].bitcast(F32)
+            g, h = divmod(b, nj // 2)
             bank = psx.tile([P, 512], F32, tag="xt", name="bank")
             for u in range(2):
                 for j2 in range(2):
-                    col = 512 * (2 * h + j2) + 256 * g + 128 * u
+                    col = 512 * (t0 % LD + 2 * h + j2) + 256 * g + 128 * u
                     nc.tensor.transpose(bank[:, P * (2 * u + j2) : P * (2 * u + j2 + 1)], xw[:, col : col + P], ident_f[:])
             state[("b", c, b)] = bank
 
@@ -68,86 +71,84 @@ def tile_ternarylinear_t_kernel(tc, x, weight_logits, scale, shift, noise, out):
                 out=gx[:].bitcast(F32)[:, 512 * b : 512 * (b + 1)].rearrange("p (t u) -> p t u", u=2),
                 in_=bank[:].rearrange("p (u t) -> p t u", u=2),
             )
-            if b < 2:
+            if b < S_SQ[c]:
                 nc.scalar.activation(
                     out=gs[:, 1024 * b : 1024 * (b + 1)].rearrange("p (t u e) -> p t u e", u=2, e=2),
                     in_=bank[:].bitcast(BF16).rearrange("p (u t e) -> p t u e", u=2, e=2),
                     func=ACT.Square,
                 )
 
-        def quantise(c):
+        def square(c):
             gx, gs = state[("g", c)]
-            nc.vector.tensor_tensor(out=gs[:, 2048:], in0=gx[:, 2048:], in1=gx[:, 2048:], op=ALU.mult)
-            ops = []
-            for nm, src in (("x", gx), ("s", gs)):
-                codes = cpool.tile([P, 1024], U32, tag="c" + nm, name="codes_" + nm, align_bytes=64)
-                scl = cpool.tile([P, 1024], U8, tag="p" + nm, name="scl_" + nm, align_bytes=64)
-                nc.vector.quantize_mx(out=codes[:].bitcast(FP8X4), scales=scl[:], in_=src[:])
-                ops.append((codes, scl))
-            state[("q", c)] = ops
+            lo, hi = 1024 * S_SQ[c], 1024 * SIZES[c]
+            nc.vector.tensor_tensor(out=gs[:, lo:hi], in0=gx[:, lo:hi], in1=gx[:, lo:hi], op=ALU.mult)
+
+        def quantise(c, which):
+            src = state[("g", c)][which]
+            n = SIZES[c]
+            nm = "xs"[which]
+            codes = cpool.tile([P, 1024], U32, tag="c" + nm, name="codes_" + nm, align_bytes=64)
+            scl = cpool.tile([P, 1024], U8, tag="p" + nm, name="scl_" + nm, align_bytes=64)
+            nc.vector.quantize_mx(out=codes[:, : 256 * n].bitcast(FP8X4), scales=scl[:, : 256 * n], in_=src[:, : 1024 * n])
+            state[("q", c, which)] = (codes, scl)
 
         def mx(c):
-            ops = state[("q", c)]
-            accs = {}
+            w = P * SIZES[c]
             for which in (1, 0):
-                codes, scl = ops[which]
-                acc = psa.tile([P, W], F32, tag="acc%d" % which, name="acc%d" % which)
+                codes, scl = state[("q", c, which)]
+                acc = psa.tile([P, 512], F32, tag="acc%d" % which, name="acc%d" % which)
                 for g in range(2):
                     w0 = P * (2 * which + g)
                     nc.tensor.matmul_mx(
-                        out=acc[:],
+                        out=acc[:, :w],
                         lhsT=w_codes[:, w0 : w0 + P].bitcast(FP8X4),
                         lhsT_scale=w_scales[:, w0 : w0 + P],
-                        rhs=codes[:, W * g : W * (g + 1)].bitcast(FP8X4),
-                        rhs_scale=scl[:, W * g : W * (g + 1)],
+                        rhs=codes[:, w * g : w * (g + 1)].bitcast(FP8X4),
+                        rhs_scale=scl[:, w * g : w * (g + 1)],
                         start=(g == 0),
                         stop=(g == 1),
                     )
-                accs[which] = acc
-            state[("a", c)] = accs
+                state[("a", c, which)] = acc
 
         def noise_transposes(c):
-            nt = psa.tile([P, W], BF16, tag="nt", name="nt")
-            for j in range(CH):
-                col = N_OUT * (CH * c + j)
+            nt = psa.tile([P, 512], BF16, tag="nt", name="nt")
+            for j in range(SIZES[c]):
+                col = N_OUT * (STARTS[c] + j)
                 nc.tensor.transpose(nt[:, P * j : P * (j + 1)], noise_sb[:, col : col + N_OUT], ident_b[:])
             state[("n", c)] = nt
 
-        def root(c):
-            sd = epool.tile([P, W], F32, tag="sd", name="sd")
-            nc.scalar.activation(out=sd[:], in_=state[("a", c)][1][:], func=ACT.Sqrt)
+        def root_and_mean(c):
+            w = P * SIZES[c]
+            sd = epool.tile([P, 512], F32, tag="sd", name="sd")
+            nc.scalar.activation(out=sd[:, :w], in_=state[("a", c, 1)][:, :w], func=ACT.Sqrt)
+            mm = epool.tile([P, 512], F32, tag="mm", name="mm")
+            nc.scalar.activation(
+                out=mm[:, :w], in_=state[("a", c, 0)][:, :w], func=ACT.Identity, scale=per_out[:, 0:1], bias=per_out[:, 1:2]
+            )
             state[("sd", c)] = sd
+            state[("m", c)] = mm
 
         def noise_term(c):
-            tt = epool.tile([P, W], F32, tag="tt", name="tt")
+            w = P * SIZES[c]
+            tt = epool.tile([P, 512], F32, tag="tt", name="tt")
             nc.vector.scalar_tensor_tensor(
-                out=tt[:], in0=state[("sd", c)][:], scalar=per_out[:, 0:1], in1=state[("n", c)][:], op0=ALU.mult, op1=ALU.mult
+                out=tt[:, :w], in0=state[("sd", c)][:, :w], scalar=per_out[:, 0:1], in1=state[("n", c)][:, :w], op0=ALU.mult, op1=ALU.mult
             )
             state[("t", c)] = tt
 
-        def add_mean(c):
-            z = epool.tile([P, W], F32, tag="z", name="z")
-            nc.vector.scalar_tensor_tensor(
-                out=z[:], in0=state[("a", c)][0][:], scalar=per_out[:, 0:1], in1=state[("t", c)][:], op0=ALU.mult, op1=ALU.add
-            )
-            state[("z", c)] = z
-
-        def z_transposes(c):
-            z = state[("z", c)]
-            zt = psa.tile([P, W], F32, tag="zt", name="zt")
-            for j in range(CH):
-                nc.tensor.transpose(zt[:, P * j : P * (j + 1)], z[:, P * j : P * (j + 1)], ident_f[:])
+        def join(c):
+            zt = psa.tile([P, 512], F32, tag="zt", name="zt")
+            for j in range(SIZES[c]):
+                sl = slice(P * j, P * (j + 1))
+                nc.tensor.matmul(out=zt[:, sl], lhsT=state[("m", c)][:, sl], rhs=ident_f[:], is_transpose=True, start=True, stop=False)
+                nc.tensor.matmul(out=zt[:, sl], lhsT=state[("t", c)][:, sl], rhs=ident_f[:], is_transpose=True, start=False, stop=True)
             state[("zt", c)] = zt
 
         def finish(c):
-            ot = epool.tile([P, CH, N_OUT], F32, tag="ot", name="ot")
-            nc.vector.tensor_tensor(
-                out=ot[:],
-                in0=state[("zt", c)][:].rearrange("p (t o) -> p t o", t=CH),
-                in1=shift_b[:].unsqueeze(1).to_broadcast([P, CH, N_OUT]),
-                op=ALU.add,
-            )
-            nc.sync.dma_start(out=out_v[:, W * c : W * (c + 1)], in_=ot[:].rearrange("p t o -> p (t o)"))
+            w = P * SIZES[c]
+            ot = epool.tile([P, 512], F32, tag="ot", name="ot")
+            nc.scalar.copy(out=ot[:, :w], in_=state[("zt", c)][:, :w])
+            nc.sync.dma_start(out=out_v[:, N_OUT * STARTS[c] : N_OUT * STARTS[c] + w], in_=ot[:, :w])
 
         logit = const.tile([P, 2 * K_IN], BF16)
         nc.sync.dma_start(out=logit[:], in_=weight_logits.rearrange("o i c -> o (i c)"))
@@ -161,8 +162,7 @@ def tile_ternarylinear_t_kernel(tc, x, weight_logits, scale, shift, noise, out):
         rows = const.tile([P, P], BF16)
         nc.gpsimd.memset(rows[:], 0.0)
         nc.scalar.dma_start(out=rows[0:1, :], in_=scale.rearrange("(a o) -> a o", a=1))
-        shift_b = const.tile([P, N_OUT], BF16)
-        nc.scalar.dma_start(out=shift_b[:], in_=shift.partition_broadcast(P))
+        nc.scalar.dma_start(out=rows[1:2, :], in_=shift.rearrange("(a o) -> a o", a=1))
         ident_f = const.tile([P, P], F32)
         make_identity(nc, ident_f[:])
         ident_b = const.tile([P, P], BF16)
@@ -173,18 +173,14 @@ def tile_ternarylinear_t_kernel(tc, x, weight_logits, scale, shift, noise, out):
         nc.scalar.activation(out=p_mag[:], in_=lv[:, 0], func=ACT.Sigmoid)
         sgn = const.tile([P, 2, 512], F32)
         nc.scalar.activation(out=sgn[:], in_=lv[:, 1], func=ACT.Tanh, scale=0.5)
-        sgn2 = const.tile([P, 2, 512], F32)
-        nc.scalar.activation(out=sgn2[:], in_=sgn[:], func=ACT.Square)
+        wm32 = const.tile([P, 2, 512], F32)
+        nc.vector.tensor_tensor(out=wm32[:], in0=p_mag[:], in1=sgn[:], op=ALU.mult)
+        wm_sq = const.tile([P, 2, 512], F32)
         w_bf = const.tile([P, 2, 2, 512], BF16)
-        nc.vector.tensor_tensor(out=w_bf[:, 0], in0=p_mag[:], in1=sgn[:], op=ALU.mult)
-        rest = const.tile([P, 2, 512], F32)
-        nc.vector.tensor_tensor(out=rest[:], in0=p_mag[:], in1=sgn2[:], op=ALU.mult)
-        nc.vector.tensor_scalar(out=rest[:], in0=rest[:], scalar1=-1.0, scalar2=1.0, op0=ALU.mult, op1=ALU.add)
-        nc.vector.tensor_tensor(out=w_bf[:, 1], in0=p_mag[:], in1=rest[:], op=ALU.mult)
         w_grp = const.tile([P, 2, 2, N_OUT, 4], BF16, align_bytes=64)
         w_codes = const.tile([P, 4 * N_OUT], U32, align_bytes=64)
         w_scales = const.tile([P, 4 * N_OUT], U8, align_bytes=64)
-        per_out = const.tile([P, 1], F32)
+        per_out = const.tile([P, 2], F32)
 
         def weight_transposes():
             for which in range(2):
@@ -198,48 +194,54 @@ def tile_ternarylinear_t_kernel(tc, x, weight_logits, scale, shift, noise, out):
             state["rt"] = rt
 
         def weight_quantise():
-            for which in range(2):
-                nc.vector.tensor_copy(out=w_grp[:, which], in_=state[("wt", which)][:].rearrange("p (g t) o -> p g o t", t=4))
-            nc.vector.tensor_copy(out=per_out[:], in_=state["rt"][:, 0:1])
+            nc.scalar.copy(out=w_grp[:, 1], in_=state[("wt", 1)][:].rearrange("p (g t) o -> p g o t", t=4))
+            nc.vector.tensor_copy(out=w_grp[:, 0], in_=state[("wt", 0)][:].rearrange("p (g t) o -> p g o t", t=4))
+            nc.vector.tensor_copy(out=per_out[:], in_=state["rt"][:, 0:2])
             nc.vector.quantize_mx(
                 out=w_codes[:].bitcast(FP8X4),
                 scales=w_scales[:],
                 in_=w_grp[:].rearrange("p w g o t -> p (w g o t)"),
             )
 
-        for b in range(4):
+        for b in range(SIZES[0]):
             x_transposes(0, b)
 
         def live(c):
             return 0 <= c < NCH
 
         for s in range(NCH + 3):
-            if live(s + 4):
-                load(s + 4)
+            if live(s) and STARTS[s] % LD == 0 and STARTS[s] // LD + 4 < T // LD:
+                load(STARTS[s] // LD + 4)
             if s in (2, 6, 10):
                 load_noise((s + 2) // 4)
+            if s == 2:
+                weight_quantise()
             if live(s - 2):
                 mx(s - 2)
             if live(s - 3):
-                z_transposes(s - 3)
+                join(s - 3)
             if live(s - 2):
                 noise_transposes(s - 2)
             for b in range(4):
-                if live(s):
+                if live(s) and b < SIZES[s]:
                     front_bank(s, b)
-                if live(s + 1):
+                if live(s + 1) and b < SIZES[s + 1]:
                     x_transposes(s + 1, b)
                 if b == 1 and live(s - 2):
-                    root(s - 2)
-                if b == 1 and s == 0:
-                    weight_transposes()
+                    root_and_mean(s - 2)
             if s == 0:
-                weight_quantise()
-            if live(s - 1):
-                quantise(s - 1)
-            if live(s - 2):
-                noise_term(s - 2)
+                nc.scalar.activation(out=wm_sq[:], in_=wm32[:], func=ACT.Square)
+                nc.scalar.copy(out=w_bf[:, 0], in_=wm32[:])
             if live(s - 3):
                 finish(s - 3)
+            if live(s - 1):
+                square(s - 1)
+                quantise(s - 1, 0)
+            if s == 1:
+                nc.vector.tensor_tensor(out=w_bf[:, 1], in0=p_mag[:], in1=wm_sq[:], op=ALU.subtract)
+            if live(s - 1):
+                quantise(s - 1, 1)
             if live(s - 2):
-                add_mean(s - 2)
+                noise_term(s - 2)
+            if s == 1:
+                weight_transposes()

@@ -19,7 +19,7 @@ LD = 4
 SIZES = [4, 4, 4, 4, 4, 4, 4, 4, 4, 4, 4, 4, 4, 4, 4, 2, 2]
 STARTS = [0, 4, 8, 12, 16, 20, 24, 28, 32, 36, 40, 44, 48, 52, 56, 60, 62]
 NCH = len(SIZES)
-S_SQ = [0, 0, 1, 0, 1, 0, 1, 0, 1, 0, 1, 1, 1, 1, 2, 1, 1]
+S_SQ = [0, 1, 1, 0, 1, 1, 0, 1, 1, 0, 1, 1, 0, 1, 1, 1, 1]
 
 
 def tile_ternarylinear_t_kernel(tc, x, weight_logits, scale, shift, noise, out):
@@ -167,16 +167,22 @@ def tile_ternarylinear_t_kernel(tc, x, weight_logits, scale, shift, noise, out):
         make_identity(nc, ident_f[:])
         ident_b = const.tile([P, P], BF16)
         make_identity(nc, ident_b[:])
+        warm = const.tile([P, 2], F32)
+        nc.gpsimd.memset(warm[:], 1.0)
 
         lv = logit[:].rearrange("o (j e c) -> o c e j", e=2, c=2)
         p_mag = const.tile([P, 2, 512], F32)
         nc.scalar.activation(out=p_mag[:], in_=lv[:, 0], func=ACT.Sigmoid)
         sgn = const.tile([P, 2, 512], F32)
         nc.scalar.activation(out=sgn[:], in_=lv[:, 1], func=ACT.Tanh, scale=0.5)
+        nc.scalar.activation(out=warm[:, 1:2], in_=warm[:, 0:1], func=ACT.Sqrt)
         wm32 = const.tile([P, 2, 512], F32)
         nc.vector.tensor_tensor(out=wm32[:], in0=p_mag[:], in1=sgn[:], op=ALU.mult)
         wm_sq = const.tile([P, 2, 512], F32)
+        nc.vector.tensor_tensor(out=wm_sq[:], in0=wm32[:], in1=wm32[:], op=ALU.mult)
         w_bf = const.tile([P, 2, 2, 512], BF16)
+        nc.vector.tensor_tensor(out=w_bf[:, 1], in0=p_mag[:], in1=wm_sq[:], op=ALU.subtract)
+        nc.vector.tensor_copy(out=w_bf[:, 0], in_=wm32[:])
         w_grp = const.tile([P, 2, 2, N_OUT, 4], BF16, align_bytes=64)
         w_codes = const.tile([P, 4 * N_OUT], U32, align_bytes=64)
         w_scales = const.tile([P, 4 * N_OUT], U8, align_bytes=64)
@@ -193,9 +199,11 @@ def tile_ternarylinear_t_kernel(tc, x, weight_logits, scale, shift, noise, out):
             nc.tensor.transpose(rt[:], rows[:], ident_b[:])
             state["rt"] = rt
 
+        def weight_copies():
+            for which in (1, 0):
+                nc.scalar.copy(out=w_grp[:, which], in_=state[("wt", which)][:].rearrange("p (g t) o -> p g o t", t=4))
+
         def weight_quantise():
-            nc.scalar.copy(out=w_grp[:, 1], in_=state[("wt", 1)][:].rearrange("p (g t) o -> p g o t", t=4))
-            nc.vector.tensor_copy(out=w_grp[:, 0], in_=state[("wt", 0)][:].rearrange("p (g t) o -> p g o t", t=4))
             nc.vector.tensor_copy(out=per_out[:], in_=state["rt"][:, 0:2])
             nc.vector.quantize_mx(
                 out=w_codes[:].bitcast(FP8X4),
@@ -214,8 +222,8 @@ def tile_ternarylinear_t_kernel(tc, x, weight_logits, scale, shift, noise, out):
                 load(STARTS[s] // LD + 4)
             if s in (2, 6, 10):
                 load_noise((s + 2) // 4)
-            if s == 2:
-                weight_quantise()
+            if live(s - 3):
+                noise_term(s - 3)
             if live(s - 2):
                 mx(s - 2)
             if live(s - 3):
@@ -227,21 +235,17 @@ def tile_ternarylinear_t_kernel(tc, x, weight_logits, scale, shift, noise, out):
                     front_bank(s, b)
                 if live(s + 1) and b < SIZES[s + 1]:
                     x_transposes(s + 1, b)
-                if b == 1 and live(s - 2):
-                    root_and_mean(s - 2)
-            if s == 0:
-                nc.scalar.activation(out=wm_sq[:], in_=wm32[:], func=ACT.Square)
-                nc.scalar.copy(out=w_bf[:, 0], in_=wm32[:])
+            if s == 1:
+                weight_copies()
+            if live(s - 2):
+                root_and_mean(s - 2)
             if live(s - 3):
                 finish(s - 3)
+            if s == 0:
+                weight_transposes()
             if live(s - 1):
                 square(s - 1)
                 quantise(s - 1, 0)
-            if s == 1:
-                nc.vector.tensor_tensor(out=w_bf[:, 1], in0=p_mag[:], in1=wm_sq[:], op=ALU.subtract)
-            if live(s - 1):
                 quantise(s - 1, 1)
-            if live(s - 2):
-                noise_term(s - 2)
             if s == 1:
-                weight_transposes()
+                weight_quantise()

@@ -19,7 +19,7 @@ LD = 4
 SIZES = [4, 4, 4, 4, 4, 4, 4, 4, 4, 4, 4, 4, 4, 4, 4, 2, 2]
 STARTS = [0, 4, 8, 12, 16, 20, 24, 28, 32, 36, 40, 44, 48, 52, 56, 60, 62]
 NCH = len(SIZES)
-S_SQ = [0, 1, 1, 0, 1, 1, 0, 1, 1, 0, 1, 1, 0, 1, 1, 1, 1]
+S_SQ = [0, 1, 1, 1, 1, 1, 1, 1, 1, 1, 1, 1, 1, 1, 1, 1, 1]
 
 
 def tile_ternarylinear_t_kernel(tc, x, weight_logits, scale, shift, noise, out):

@@ -19,7 +19,7 @@ LD = 4
 SIZES = [4, 4, 4, 4, 4, 4, 4, 4, 4, 4, 4, 4, 4, 4, 4, 2, 2]
 STARTS = [0, 4, 8, 12, 16, 20, 24, 28, 32, 36, 40, 44, 48, 52, 56, 60, 62]
 NCH = len(SIZES)
-S_SQ = [0, 1, 1, 1, 1, 1, 1, 1, 1, 1, 1, 1, 1, 1, 1, 1, 1]
+S_SQ = [0, 1, 1, 1, 1, 1, 0, 1, 1, 1, 1, 1, 0, 1, 1, 1, 1]
 
 
 def tile_ternarylinear_t_kernel(tc, x, weight_logits, scale, shift, noise, out):

@@ -36,7 +36,6 @@ def tile_ternarylinear_t_kernel(tc, x, weight_logits, scale, shift, noise, out):
         epool = ctx.enter_context(tc.tile_pool(name="epool", bufs=3))
         psx = ctx.enter_context(tc.psum_pool(name="psx", bufs=4))
         psa = ctx.enter_context(tc.psum_pool(name="psa", bufs=1))
-        ctx.enter_context(tc.manual_schedule())
 
         state = {}
 

@@ -15,11 +15,11 @@ N_TOK, K_IN, N_OUT = 8192, 1024, 128
 FLOPS = 2 * 2 * N_TOK * K_IN * N_OUT
 P = 128
 T = N_TOK // P
-LD = 4
-SIZES = [4, 4, 4, 4, 4, 4, 4, 4, 4, 4, 4, 4, 4, 4, 4, 2, 2]
-STARTS = [0, 4, 8, 12, 16, 20, 24, 28, 32, 36, 40, 44, 48, 52, 56, 60, 62]
-NCH = len(SIZES)
-S_SQ = [0, 1, 1, 1, 1, 1, 0, 1, 1, 1, 1, 1, 0, 1, 1, 1, 1]
+SIZES = [1, 1, 2] + [4] * 14 + [2, 2]
+STARTS = [sum(SIZES[:i]) for i in range(len(SIZES))]
+GROUPS = [[0, 1, 2]] + [[i] for i in range(3, len(SIZES))]
+NGR = len(GROUPS)
+SHARES = {0: [("W", 0, 256)], 1: [("W", 0, 256)], 2: [("W", 0, 256)], 3: [("S", 64, 256), ("W", 0, 64)]}
 
 
 def tile_ternarylinear_t_kernel(tc, x, weight_logits, scale, shift, noise, out):
@@ -29,166 +29,202 @@ def tile_ternarylinear_t_kernel(tc, x, weight_logits, scale, shift, noise, out):
     out_v = out.rearrange("(p t) o -> p (t o)", t=T)
 
     with ExitStack() as ctx:
+        ctx.enter_context(tc.manual_schedule())
         const = ctx.enter_context(tc.tile_pool(name="const", bufs=1))
-        xpool = ctx.enter_context(tc.tile_pool(name="xpool", bufs=4))
-        gpool = ctx.enter_context(tc.tile_pool(name="gpool", bufs=3))
-        cpool = ctx.enter_context(tc.tile_pool(name="cpool", bufs=3))
+        xpool = ctx.enter_context(tc.tile_pool(name="xpool", bufs=6))
+        gxpool = ctx.enter_context(tc.tile_pool(name="gxpool", bufs=3))
+        gspool = ctx.enter_context(tc.tile_pool(name="gspool", bufs=2))
+        cpool = ctx.enter_context(tc.tile_pool(name="cpool", bufs=4))
         epool = ctx.enter_context(tc.tile_pool(name="epool", bufs=3))
         psx = ctx.enter_context(tc.psum_pool(name="psx", bufs=4))
         psa = ctx.enter_context(tc.psum_pool(name="psa", bufs=1))
 
         state = {}
 
-        def load(q):
-            xt = xpool.tile([P, LD * K_IN], BF16, tag="x", name="xt")
-            nc.sync.dma_start(out=xt[:], in_=x_v[:, LD * K_IN * q : LD * K_IN * (q + 1)])
-            state[("x", q)] = xt
+        def load(i):
+            n, t0 = SIZES[i], STARTS[i]
+            xt = xpool.tile([P, 4 * K_IN], BF16, tag="x", name="xt")
+            nc.sync.dma_start(out=xt[:, : n * K_IN], in_=x_v[:, K_IN * t0 : K_IN * (t0 + n)])
+            state[("x", i)] = xt
 
         def load_noise(q):
             w = T * N_OUT // 4
             nc.sync.dma_start(out=noise_sb[:, w * q : w * (q + 1)], in_=noise_v[:, w * q : w * (q + 1)])
 
-        def x_transposes(c, b):
-            t0, nj = STARTS[c], SIZES[c]
-            xw = state[("x", t0 // LD)][:].bitcast(F32)
-            g, h = divmod(b, nj // 2)
+        def x_transposes(i, b):
+            n = SIZES[i]
+            xw = state[("x", i)][:].bitcast(F32)
             bank = psx.tile([P, 512], F32, tag="xt", name="bank")
-            for u in range(2):
-                for j2 in range(2):
-                    col = 512 * (t0 % LD + 2 * h + j2) + 256 * g + 128 * u
-                    nc.tensor.transpose(bank[:, P * (2 * u + j2) : P * (2 * u + j2 + 1)], xw[:, col : col + P], ident_f[:])
-            state[("b", c, b)] = bank
+            for q in range(4):
+                if n == 1:
+                    col = P * q
+                else:
+                    g, h = divmod(b, n // 2)
+                    u, j2 = divmod(q, 2)
+                    col = 512 * (2 * h + j2) + 256 * g + 128 * u
+                nc.tensor.transpose(bank[:, P * q : P * (q + 1)], xw[:, col : col + P], ident_f[:])
+            state[("b", i, b)] = bank
 
-        def front_bank(c, b):
+        def bank_copy(i, b):
             if b == 0:
-                gx_new = gpool.tile([P, 4096], BF16, tag="gx", name="gx", align_bytes=64)
-                gs_new = gpool.tile([P, 4096], BF16, tag="gs", name="gs", align_bytes=64)
-                state[("g", c)] = (gx_new, gs_new)
-            gx, gs = state[("g", c)]
-            bank = state[("b", c, b)]
-            nc.scalar.copy(
-                out=gx[:].bitcast(F32)[:, 512 * b : 512 * (b + 1)].rearrange("p (t u) -> p t u", u=2),
-                in_=bank[:].rearrange("p (u t) -> p t u", u=2),
-            )
-            if b < S_SQ[c]:
-                nc.scalar.activation(
-                    out=gs[:, 1024 * b : 1024 * (b + 1)].rearrange("p (t u e) -> p t u e", u=2, e=2),
-                    in_=bank[:].bitcast(BF16).rearrange("p (u t e) -> p t u e", u=2, e=2),
-                    func=ACT.Square,
+                state[("gx", i)] = gxpool.tile([P, 4096], BF16, tag="gx", name="gx", align_bytes=64)
+            gx = state[("gx", i)]
+            bank = state[("b", i, b)]
+            words = gx[:].bitcast(F32)[:, 512 * b : 512 * (b + 1)]
+            if SIZES[i] == 1:
+                nc.scalar.copy(
+                    out=words.rearrange("p (g t u) -> p g t u", g=2, u=2), in_=bank[:].rearrange("p (g u t) -> p g t u", g=2, u=2)
                 )
+            else:
+                nc.scalar.copy(out=words.rearrange("p (t u) -> p t u", u=2), in_=bank[:].rearrange("p (u t) -> p t u", u=2))
 
-        def square(c):
-            gx, gs = state[("g", c)]
-            lo, hi = 1024 * S_SQ[c], 1024 * SIZES[c]
+        def new_squares(i):
+            state[("gs", i)] = gspool.tile([P, 4096], BF16, tag="gs", name="gs", align_bytes=64)
+
+        def square_plain(i, lo, hi):
+            gx, gs = state[("gx", i)], state[("gs", i)]
             nc.vector.tensor_tensor(out=gs[:, lo:hi], in0=gx[:, lo:hi], in1=gx[:, lo:hi], op=ALU.mult)
 
-        def quantise(c, which):
-            src = state[("g", c)][which]
-            n = SIZES[c]
+        def square(i, b, who, lo, hi):
+            gx, gs = state[("gx", i)], state[("gs", i)]
+            a, z = 1024 * b + 4 * lo, 1024 * b + 4 * hi
+            quads = state[("b", i, b)][:].bitcast(BF16).rearrange("p (u t e) -> p t u e", u=2, e=2)[:, lo:hi]
+            if who == "G":
+                nc.gpsimd.tensor_tensor(out=gs[:, a:z], in0=gx[:, a:z], in1=gx[:, a:z], op=ALU.mult)
+            elif who == "W":
+                nc.vector.tensor_tensor(out=gs[:, a:z], in0=gx[:, a:z], in1=gx[:, a:z], op=ALU.mult)
+            elif who == "V":
+                nc.vector.tensor_tensor(
+                    out=gs[:, a:z].rearrange("p (t u e) -> p t u e", u=2, e=2),
+                    in0=quads,
+                    in1=gx[:, a:z].rearrange("p (t u e) -> p t u e", u=2, e=2),
+                    op=ALU.mult,
+                )
+            else:
+                nc.scalar.activation(out=gs[:, a:z].rearrange("p (t u e) -> p t u e", u=2, e=2), in_=quads, func=ACT.Square)
+
+        def quantise(i, which):
+            src = state[(("gx", "gs")[which], i)]
+            n = SIZES[i]
             nm = "xs"[which]
             codes = cpool.tile([P, 1024], U32, tag="c" + nm, name="codes_" + nm, align_bytes=64)
             scl = cpool.tile([P, 1024], U8, tag="p" + nm, name="scl_" + nm, align_bytes=64)
             nc.vector.quantize_mx(out=codes[:, : 256 * n].bitcast(FP8X4), scales=scl[:, : 256 * n], in_=src[:, : 1024 * n])
-            state[("q", c, which)] = (codes, scl)
+            state[("q", i, which)] = (codes, scl)
 
-        def mx(c):
-            w = P * SIZES[c]
+        def tiles(k):
+            return sum(SIZES[i] for i in GROUPS[k])
+
+        def first(k):
+            return STARTS[GROUPS[k][0]]
+
+        def mx(k):
             for which in (1, 0):
-                codes, scl = state[("q", c, which)]
                 acc = psa.tile([P, 512], F32, tag="acc%d" % which, name="acc%d" % which)
-                for g in range(2):
-                    w0 = P * (2 * which + g)
-                    nc.tensor.matmul_mx(
-                        out=acc[:, :w],
-                        lhsT=w_codes[:, w0 : w0 + P].bitcast(FP8X4),
-                        lhsT_scale=w_scales[:, w0 : w0 + P],
-                        rhs=codes[:, w * g : w * (g + 1)].bitcast(FP8X4),
-                        rhs_scale=scl[:, w * g : w * (g + 1)],
-                        start=(g == 0),
-                        stop=(g == 1),
-                    )
-                state[("a", c, which)] = acc
+                for i in GROUPS[k]:
+                    codes, scl = state[("q", i, which)]
+                    w = P * SIZES[i]
+                    o = P * (STARTS[i] - first(k))
+                    for g in range(2):
+                        w0 = P * (2 * which + g)
+                        nc.tensor.matmul_mx(
+                            out=acc[:, o : o + w],
+                            lhsT=w_codes[:, w0 : w0 + P].bitcast(FP8X4),
+                            lhsT_scale=w_scales[:, w0 : w0 + P],
+                            rhs=codes[:, w * g : w * (g + 1)].bitcast(FP8X4),
+                            rhs_scale=scl[:, w * g : w * (g + 1)],
+                            start=(g == 0),
+                            stop=(g == 1),
+                        )
+                state[("a", k, which)] = acc
 
-        def noise_transposes(c):
+        def noise_transposes(k):
             nt = psa.tile([P, 512], BF16, tag="nt", name="nt")
-            for j in range(SIZES[c]):
-                col = N_OUT * (STARTS[c] + j)
+            for j in range(tiles(k)):
+                col = N_OUT * (first(k) + j)
                 nc.tensor.transpose(nt[:, P * j : P * (j + 1)], noise_sb[:, col : col + N_OUT], ident_b[:])
-            state[("n", c)] = nt
+            state[("n", k)] = nt
 
-        def root_and_mean(c):
-            w = P * SIZES[c]
+        def root_and_mean(k):
+            w = P * tiles(k)
             sd = epool.tile([P, 512], F32, tag="sd", name="sd")
-            nc.scalar.activation(out=sd[:, :w], in_=state[("a", c, 1)][:, :w], func=ACT.Sqrt)
+            nc.scalar.activation(out=sd[:, :w], in_=state[("a", k, 1)][:, :w], func=ACT.Sqrt)
             mm = epool.tile([P, 512], F32, tag="mm", name="mm")
             nc.scalar.activation(
-                out=mm[:, :w], in_=state[("a", c, 0)][:, :w], func=ACT.Identity, scale=per_out[:, 0:1], bias=per_out[:, 1:2]
+                out=mm[:, :w], in_=state[("a", k, 0)][:, :w], func=ACT.Identity, scale=per_out[:, 0:1], bias=per_out[:, 1:2]
             )
-            state[("sd", c)] = sd
-            state[("m", c)] = mm
+            state[("sd", k)] = sd
+            state[("m", k)] = mm
 
-        def noise_term(c):
-            w = P * SIZES[c]
+        def noise_term(k):
+            w = P * tiles(k)
             tt = epool.tile([P, 512], F32, tag="tt", name="tt")
             nc.vector.scalar_tensor_tensor(
-                out=tt[:, :w], in0=state[("sd", c)][:, :w], scalar=per_out[:, 0:1], in1=state[("n", c)][:, :w], op0=ALU.mult, op1=ALU.mult
+                out=tt[:, :w], in0=state[("sd", k)][:, :w], scalar=per_out[:, 0:1], in1=state[("n", k)][:, :w], op0=ALU.mult, op1=ALU.mult
             )
-            state[("t", c)] = tt
+            state[("t", k)] = tt
 
-        def join(c):
+        def join(k):
             zt = psa.tile([P, 512], F32, tag="zt", name="zt")
-            for j in range(SIZES[c]):
+            for j in range(tiles(k)):
                 sl = slice(P * j, P * (j + 1))
-                nc.tensor.matmul(out=zt[:, sl], lhsT=state[("m", c)][:, sl], rhs=ident_f[:], is_transpose=True, start=True, stop=False)
-                nc.tensor.matmul(out=zt[:, sl], lhsT=state[("t", c)][:, sl], rhs=ident_f[:], is_transpose=True, start=False, stop=True)
-            state[("zt", c)] = zt
+                nc.tensor.matmul(out=zt[:, sl], lhsT=state[("m", k)][:, sl], rhs=ident_f[:], is_transpose=True, start=True, stop=False)
+                nc.tensor.matmul(out=zt[:, sl], lhsT=state[("t", k)][:, sl], rhs=ident_f[:], is_transpose=True, start=False, stop=True)
+            state[("zt", k)] = zt
 
-        def finish(c):
-            w = P * SIZES[c]
+        def finish(k):
+            w = P * tiles(k)
             ot = epool.tile([P, 512], F32, tag="ot", name="ot")
-            nc.scalar.copy(out=ot[:, :w], in_=state[("zt", c)][:, :w])
-            nc.sync.dma_start(out=out_v[:, N_OUT * STARTS[c] : N_OUT * STARTS[c] + w], in_=ot[:, :w])
+            nc.scalar.copy(out=ot[:, :w], in_=state[("zt", k)][:, :w])
+            nc.sync.dma_start(out=out_v[:, N_OUT * first(k) : N_OUT * first(k) + w], in_=ot[:, :w])
 
         logit = const.tile([P, 2 * K_IN], BF16)
-        nc.sync.dma_start(out=logit[:], in_=weight_logits.rearrange("o i c -> o (i c)"))
         noise_sb = const.tile([P, T * N_OUT], BF16)
         load(0)
         load(1)
-        load_noise(0)
+        nc.sync.dma_start(out=logit[:], in_=weight_logits.rearrange("o i c -> o (i c)"))
         load(2)
         load(3)
+        load_noise(0)
+        load(4)
+        load(5)
 
-        rows = const.tile([P, P], BF16)
-        nc.gpsimd.memset(rows[:], 0.0)
-        nc.scalar.dma_start(out=rows[0:1, :], in_=scale.rearrange("(a o) -> a o", a=1))
-        nc.scalar.dma_start(out=rows[1:2, :], in_=shift.rearrange("(a o) -> a o", a=1))
+        warm = const.tile([P, 3], F32)
+        nc.gpsimd.memset(warm[:], 1.0)
         ident_f = const.tile([P, P], F32)
         make_identity(nc, ident_f[:])
         ident_b = const.tile([P, P], BF16)
         make_identity(nc, ident_b[:])
-        warm = const.tile([P, 2], F32)
-        nc.gpsimd.memset(warm[:], 1.0)
+        rows = const.tile([P, P], BF16)
+        nc.gpsimd.memset(rows[:], 0.0)
+        nc.scalar.activation(out=warm[:, 2:3], in_=warm[:, 0:1], func=ACT.Sigmoid)
+        nc.sync.dma_start(out=rows[0:1, :], in_=scale.rearrange("(a o) -> a o", a=1))
+        nc.sync.dma_start(out=rows[1:2, :], in_=shift.rearrange("(a o) -> a o", a=1))
 
         lv = logit[:].rearrange("o (j e c) -> o c e j", e=2, c=2)
         p_mag = const.tile([P, 2, 512], F32)
-        nc.scalar.activation(out=p_mag[:], in_=lv[:, 0], func=ACT.Sigmoid)
         sgn = const.tile([P, 2, 512], F32)
-        nc.scalar.activation(out=sgn[:], in_=lv[:, 1], func=ACT.Tanh, scale=0.5)
-        nc.scalar.activation(out=warm[:, 1:2], in_=warm[:, 0:1], func=ACT.Sqrt)
         wm32 = const.tile([P, 2, 512], F32)
-        nc.vector.tensor_tensor(out=wm32[:], in0=p_mag[:], in1=sgn[:], op=ALU.mult)
         wm_sq = const.tile([P, 2, 512], F32)
-        nc.vector.tensor_tensor(out=wm_sq[:], in0=wm32[:], in1=wm32[:], op=ALU.mult)
         w_bf = const.tile([P, 2, 2, 512], BF16)
-        nc.vector.tensor_tensor(out=w_bf[:, 1], in0=p_mag[:], in1=wm_sq[:], op=ALU.subtract)
-        nc.vector.tensor_copy(out=w_bf[:, 0], in_=wm32[:])
         w_grp = const.tile([P, 2, 2, N_OUT, 4], BF16, align_bytes=64)
         w_codes = const.tile([P, 4 * N_OUT], U32, align_bytes=64)
         w_scales = const.tile([P, 4 * N_OUT], U8, align_bytes=64)
         per_out = const.tile([P, 2], F32)
 
+        def weight_sigmoids():
+            nc.scalar.activation(out=p_mag[:], in_=lv[:, 0], func=ACT.Sigmoid)
+            nc.scalar.activation(out=sgn[:], in_=lv[:, 1], func=ACT.Tanh, scale=0.5)
+            nc.scalar.activation(out=warm[:, 1:2], in_=warm[:, 0:1], func=ACT.Sqrt)
+
+        def weight_values():
+            nc.vector.tensor_tensor(out=wm32[:], in0=p_mag[:], in1=sgn[:], op=ALU.mult)
+            nc.vector.tensor_tensor(out=wm_sq[:], in0=wm32[:], in1=wm32[:], op=ALU.mult)
+            nc.vector.tensor_tensor(out=w_bf[:, 1], in0=p_mag[:], in1=wm_sq[:], op=ALU.subtract)
+            nc.vector.tensor_copy(out=w_bf[:, 0], in_=wm32[:])
+
         def weight_transposes():
-            for which in range(2):
+            for which in (1, 0):
                 wt = psa.tile([P, 8, P], BF16, tag="acc%d" % which, name="wt%d" % which)
                 for m in range(4):
                     for e in range(2):
@@ -210,41 +246,61 @@ def tile_ternarylinear_t_kernel(tc, x, weight_logits, scale, shift, noise, out):
                 in_=w_grp[:].rearrange("p w g o t -> p (w g o t)"),
             )
 
-        for b in range(SIZES[0]):
-            x_transposes(0, b)
+        def live(k):
+            return 0 <= k < NGR
 
-        def live(c):
-            return 0 <= c < NCH
+        def small(i):
+            new_squares(i)
+            square_plain(i, 0, 1024 * SIZES[i])
+            quantise(i, 0)
+            quantise(i, 1)
 
-        for s in range(NCH + 3):
-            if live(s) and STARTS[s] % LD == 0 and STARTS[s] // LD + 4 < T // LD:
-                load(STARTS[s] // LD + 4)
+        for i in range(3):
+            for b in range(SIZES[i]):
+                x_transposes(i, b)
+        bank_copy(0, 0)
+        small(0)
+        bank_copy(1, 0)
+        small(1)
+        weight_sigmoids()
+        bank_copy(2, 0)
+        bank_copy(2, 1)
+        for b in range(4):
+            x_transposes(3, b)
+        weight_values()
+        small(2)
+
+        for s in range(1, NGR + 3):
+            i = s + 2
+            if i + 3 < len(SIZES):
+                load(i + 3)
             if s in (2, 6, 10):
                 load_noise((s + 2) // 4)
-            if live(s - 3):
-                noise_term(s - 3)
+            if live(s - 1) and s > 1:
+                for which in (0, 1) if live(s + 1) else (1, 0):
+                    quantise(i - 1, which)
             if live(s - 2):
                 mx(s - 2)
             if live(s - 3):
                 join(s - 3)
             if live(s - 2):
                 noise_transposes(s - 2)
-            for b in range(4):
-                if live(s) and b < SIZES[s]:
-                    front_bank(s, b)
-                if live(s + 1) and b < SIZES[s + 1]:
-                    x_transposes(s + 1, b)
+            if live(s):
+                new_squares(i)
+                n = SIZES[i]
+                for b in range(n):
+                    bank_copy(i, b)
+                    for who, lo, hi in SHARES[b] if n == 4 else [("V", 0, 256)] if n == 2 else [("W", 0, 256)]:
+                        square(i, b, who, lo, hi)
+                    if live(s + 1) and b < SIZES[i + 1]:
+                        x_transposes(i + 1, b)
+                    if s == 1 and b == 0:
+                        weight_transposes()
             if s == 1:
                 weight_copies()
+                weight_quantise()
             if live(s - 2):
                 root_and_mean(s - 2)
+                noise_term(s - 2)
             if live(s - 3):
                 finish(s - 3)
-            if s == 0:
-                weight_transposes()
-            if live(s - 1):
-                square(s - 1)
-                quantise(s - 1, 0)
-                quantise(s - 1, 1)
-            if s == 1:
-                weight_quantise()

@@ -19,7 +19,7 @@ SIZES = [1, 1, 2] + [4] * 14 + [2, 2]
 STARTS = [sum(SIZES[:i]) for i in range(len(SIZES))]
 GROUPS = [[0, 1, 2]] + [[i] for i in range(3, len(SIZES))]
 NGR = len(GROUPS)
-SHARES = {0: [("W", 0, 256)], 1: [("W", 0, 256)], 2: [("W", 0, 256)], 3: [("S", 64, 256), ("W", 0, 64)]}
+S_TOK = [0] * 3 + [256, 256, 256, 0] * 4
 
 
 def tile_ternarylinear_t_kernel(tc, x, weight_logits, scale, shift, noise, out):
@@ -290,12 +290,13 @@ def tile_ternarylinear_t_kernel(tc, x, weight_logits, scale, shift, noise, out):
                 n = SIZES[i]
                 for b in range(n):
                     bank_copy(i, b)
-                    for who, lo, hi in SHARES[b] if n == 4 else [("V", 0, 256)] if n == 2 else [("W", 0, 256)]:
-                        square(i, b, who, lo, hi)
+                    if n == 4 and b == 0 and S_TOK[i] > 0:
+                        square(i, b, "S", 0, S_TOK[i])
                     if live(s + 1) and b < SIZES[i + 1]:
                         x_transposes(i + 1, b)
                     if s == 1 and b == 0:
                         weight_transposes()
+                square_plain(i, 4 * S_TOK[i] if n == 4 else 0, 1024 * n)
             if s == 1:
                 weight_copies()
                 weight_quantise()

@@ -24,9 +24,6 @@ S_TOK = [0] * 3 + [256, 256, 256, 0] * 4
 
 def tile_ternarylinear_t_kernel(tc, x, weight_logits, scale, shift, noise, out):
     nc = tc.nc
-    x_v = x.rearrange("(p t) k -> p (t k)", t=T)
-    noise_v = noise.rearrange("(p t) o -> p (t o)", t=T)
-    out_v = out.rearrange("(p t) o -> p (t o)", t=T)
 
     with ExitStack() as ctx:
         ctx.enter_context(tc.manual_schedule())
@@ -41,15 +38,29 @@ def tile_ternarylinear_t_kernel(tc, x, weight_logits, scale, shift, noise, out):
 
         state = {}
 
+        def tiles(k):
+            return sum(SIZES[i] for i in GROUPS[k])
+
+        def first(k):
+            return STARTS[GROUPS[k][0]]
+
+        def group_rows(a, k):
+            return a[P * first(k) : P * (first(k) + tiles(k)), :].rearrange("(p j) c -> p (j c)", j=tiles(k))
+
         def load(i):
             n, t0 = SIZES[i], STARTS[i]
             xt = xpool.tile([P, 4 * K_IN], BF16, tag="x", name="xt")
-            nc.sync.dma_start(out=xt[:, : n * K_IN], in_=x_v[:, K_IN * t0 : K_IN * (t0 + n)])
+            k = [g for g in range(NGR) if i in GROUPS[g]][0]
+            j = t0 - first(k)
+            rows_v = group_rows(x, k)
+            nc.sync.dma_start(out=xt[:, : n * K_IN], in_=rows_v[:, K_IN * j : K_IN * (j + n)])
             state[("x", i)] = xt
 
         def load_noise(q):
-            w = T * N_OUT // 4
-            nc.sync.dma_start(out=noise_sb[:, w * q : w * (q + 1)], in_=noise_v[:, w * q : w * (q + 1)])
+            for k in range(NGR):
+                if first(k) // (T // 4) == q:
+                    lo = N_OUT * first(k)
+                    nc.sync.dma_start(out=noise_sb[:, lo : lo + N_OUT * tiles(k)], in_=group_rows(noise, k))
 
         def x_transposes(i, b):
             n = SIZES[i]
@@ -112,12 +123,6 @@ def tile_ternarylinear_t_kernel(tc, x, weight_logits, scale, shift, noise, out):
             nc.vector.quantize_mx(out=codes[:, : 256 * n].bitcast(FP8X4), scales=scl[:, : 256 * n], in_=src[:, : 1024 * n])
             state[("q", i, which)] = (codes, scl)
 
-        def tiles(k):
-            return sum(SIZES[i] for i in GROUPS[k])
-
-        def first(k):
-            return STARTS[GROUPS[k][0]]
-
         def mx(k):
             for which in (1, 0):
                 acc = psa.tile([P, 512], F32, tag="acc%d" % which, name="acc%d" % which)
@@ -176,7 +181,7 @@ def tile_ternarylinear_t_kernel(tc, x, weight_logits, scale, shift, noise, out):
             w = P * tiles(k)
             ot = epool.tile([P, 512], F32, tag="ot", name="ot")
             nc.scalar.copy(out=ot[:, :w], in_=state[("zt", k)][:, :w])
-            nc.sync.dma_start(out=out_v[:, N_OUT * first(k) : N_OUT * first(k) + w], in_=ot[:, :w])
+            nc.sync.dma_start(out=group_rows(out, k), in_=ot[:, :w])
 
         logit = const.tile([P, 2 * K_IN], BF16)
         noise_sb = const.tile([P, T * N_OUT], BF16)

@@ -19,7 +19,7 @@ SIZES = [1, 1, 2] + [4] * 14 + [2, 2]
 STARTS = [sum(SIZES[:i]) for i in range(len(SIZES))]
 GROUPS = [[0, 1, 2]] + [[i] for i in range(3, len(SIZES))]
 NGR = len(GROUPS)
-S_TOK = [0] * 3 + [256, 256, 256, 0] * 4
+S_TOK = [0,0,0]+[192]*12+[256]*2+[256,256]
 
 
 def tile_ternarylinear_t_kernel(tc, x, weight_logits, scale, shift, noise, out):
@@ -88,6 +88,14 @@ def tile_ternarylinear_t_kernel(tc, x, weight_logits, scale, shift, noise, out):
                 )
             else:
                 nc.scalar.copy(out=words.rearrange("p (t u) -> p t u", u=2), in_=bank[:].rearrange("p (u t) -> p t u", u=2))
+
+        def first_copy():
+            gx = gxpool.tile([P, 4096], BF16, tag="gx", name="gx", align_bytes=64)
+            state[("gx", 0)] = gx
+            nc.vector.tensor_copy(
+                out=gx[:].bitcast(F32)[:, :512].rearrange("p (g t u) -> p g t u", g=2, u=2),
+                in_=state[("b", 0, 0)][:].rearrange("p (g u t) -> p g t u", g=2, u=2),
+            )
 
         def new_squares(i):
             state[("gs", i)] = gspool.tile([P, 4096], BF16, tag="gs", name="gs", align_bytes=64)
@@ -185,7 +193,11 @@ def tile_ternarylinear_t_kernel(tc, x, weight_logits, scale, shift, noise, out):
 
         logit = const.tile([P, 2 * K_IN], BF16)
         noise_sb = const.tile([P, T * N_OUT], BF16)
+        rows = const.tile([P, P], BF16)
+        nc.gpsimd.memset(rows[:], 0.0)
         load(0)
+        nc.scalar.dma_start(out=rows[0:1, :], in_=scale.rearrange("(a o) -> a o", a=1))
+        nc.scalar.dma_start(out=rows[1:2, :], in_=shift.rearrange("(a o) -> a o", a=1))
         load(1)
         nc.sync.dma_start(out=logit[:], in_=weight_logits.rearrange("o i c -> o (i c)"))
         load(2)
@@ -200,18 +212,14 @@ def tile_ternarylinear_t_kernel(tc, x, weight_logits, scale, shift, noise, out):
         make_identity(nc, ident_f[:])
         ident_b = const.tile([P, P], BF16)
         make_identity(nc, ident_b[:])
-        rows = const.tile([P, P], BF16)
-        nc.gpsimd.memset(rows[:], 0.0)
         nc.scalar.activation(out=warm[:, 2:3], in_=warm[:, 0:1], func=ACT.Sigmoid)
-        nc.sync.dma_start(out=rows[0:1, :], in_=scale.rearrange("(a o) -> a o", a=1))
-        nc.sync.dma_start(out=rows[1:2, :], in_=shift.rearrange("(a o) -> a o", a=1))
 
         lv = logit[:].rearrange("o (j e c) -> o c e j", e=2, c=2)
         p_mag = const.tile([P, 2, 512], F32)
         sgn = const.tile([P, 2, 512], F32)
         wm32 = const.tile([P, 2, 512], F32)
         wm_sq = const.tile([P, 2, 512], F32)
-        w_bf = const.tile([P, 2, 2, 512], BF16)
+        wv_bf = const.tile([P, 2, 512], BF16)
         w_grp = const.tile([P, 2, 2, N_OUT, 4], BF16, align_bytes=64)
         w_codes = const.tile([P, 4 * N_OUT], U32, align_bytes=64)
         w_scales = const.tile([P, 4 * N_OUT], U8, align_bytes=64)
@@ -225,23 +233,28 @@ def tile_ternarylinear_t_kernel(tc, x, weight_logits, scale, shift, noise, out):
         def weight_values():
             nc.vector.tensor_tensor(out=wm32[:], in0=p_mag[:], in1=sgn[:], op=ALU.mult)
             nc.vector.tensor_tensor(out=wm_sq[:], in0=wm32[:], in1=wm32[:], op=ALU.mult)
-            nc.vector.tensor_tensor(out=w_bf[:, 1], in0=p_mag[:], in1=wm_sq[:], op=ALU.subtract)
-            nc.vector.tensor_copy(out=w_bf[:, 0], in_=wm32[:])
+            nc.vector.tensor_tensor(out=wv_bf[:], in0=p_mag[:], in1=wm_sq[:], op=ALU.subtract)
 
         def weight_transposes():
-            for which in (1, 0):
-                wt = psa.tile([P, 8, P], BF16, tag="acc%d" % which, name="wt%d" % which)
-                for m in range(4):
-                    for e in range(2):
-                        nc.tensor.transpose(wt[:, 2 * m + e, :], w_bf[:, which, e, P * m : P * (m + 1)], ident_b[:])
-                state[("wt", which)] = wt
+            wt = psa.tile([P, 8, P], BF16, tag="acc1", name="wt1")
+            for m in range(4):
+                for e in range(2):
+                    nc.tensor.transpose(wt[:, 2 * m + e, :], wv_bf[:, e, P * m : P * (m + 1)], ident_b[:])
+            state[("wt", 1)] = wt
+            for g, tag in enumerate(("acc0", "zt")):
+                wt = psa.tile([P, 4, P], F32, tag=tag, name="wt0")
+                for q in range(4):
+                    m, e = divmod(4 * g + q, 2)
+                    nc.tensor.transpose(wt[:, q, :], wm32[:, e, P * m : P * (m + 1)], ident_f[:])
+                state[("wt", 0, g)] = wt
             rt = psa.tile([P, P], BF16, tag="nt", name="rt")
             nc.tensor.transpose(rt[:], rows[:], ident_b[:])
             state["rt"] = rt
 
         def weight_copies():
-            for which in (1, 0):
-                nc.scalar.copy(out=w_grp[:, which], in_=state[("wt", which)][:].rearrange("p (g t) o -> p g o t", t=4))
+            nc.scalar.copy(out=w_grp[:, 1], in_=state[("wt", 1)][:].rearrange("p (g t) o -> p g o t", t=4))
+            for g in range(2):
+                nc.scalar.copy(out=w_grp[:, 0, g], in_=state[("wt", 0, g)][:].rearrange("p t o -> p o t"))
 
         def weight_quantise():
             nc.vector.tensor_copy(out=per_out[:], in_=state["rt"][:, 0:2])
@@ -263,7 +276,7 @@ def tile_ternarylinear_t_kernel(tc, x, weight_logits, scale, shift, noise, out):
         for i in range(3):
             for b in range(SIZES[i]):
                 x_transposes(i, b)
-        bank_copy(0, 0)
+        first_copy()
         small(0)
         bank_copy(1, 0)
         small(1)
@@ -274,6 +287,8 @@ def tile_ternarylinear_t_kernel(tc, x, weight_logits, scale, shift, noise, out):
             x_transposes(3, b)
         weight_values()
         small(2)
+
+        weight_transposes()
 
         for s in range(1, NGR + 3):
             i = s + 2
@@ -290,20 +305,21 @@ def tile_ternarylinear_t_kernel(tc, x, weight_logits, scale, shift, noise, out):
                 join(s - 3)
             if live(s - 2):
                 noise_transposes(s - 2)
-            if live(s):
+            n = SIZES[i] if live(s) else 0
+            if n:
                 new_squares(i)
-                n = SIZES[i]
-                for b in range(n):
+            for b in range(4):
+                if b < n:
                     bank_copy(i, b)
-                    if n == 4 and b == 0 and S_TOK[i] > 0:
+                    if b == 0 and S_TOK[i] > 0:
                         square(i, b, "S", 0, S_TOK[i])
-                    if live(s + 1) and b < SIZES[i + 1]:
-                        x_transposes(i + 1, b)
-                    if s == 1 and b == 0:
-                        weight_transposes()
-                square_plain(i, 4 * S_TOK[i] if n == 4 else 0, 1024 * n)
+                if live(s + 1) and b < SIZES[i + 1]:
+                    x_transposes(i + 1, b)
+                if s == 1 and b == 3:
+                    weight_copies()
+            if n:
+                square_plain(i, 4 * S_TOK[i], 1024 * n)
             if s == 1:
-                weight_copies()
                 weight_quantise()
             if live(s - 2):
                 root_and_mean(s - 2)

@@ -19,7 +19,7 @@ SIZES = [1, 1, 2] + [4] * 14 + [2, 2]
 STARTS = [sum(SIZES[:i]) for i in range(len(SIZES))]
 GROUPS = [[0, 1, 2]] + [[i] for i in range(3, len(SIZES))]
 NGR = len(GROUPS)
-S_TOK = [0,0,0]+[192]*12+[256]*2+[256,256]
+S_TOK = [0,0,0]+[208]*12+[256]*2+[256,256]
 
 
 def tile_ternarylinear_t_kernel(tc, x, weight_logits, scale, shift, noise, out):
@@ -133,7 +133,10 @@ def tile_ternarylinear_t_kernel(tc, x, weight_logits, scale, shift, noise, out):
 
         def mx(k):
             for which in (1, 0):
-                acc = psa.tile([P, 512], F32, tag="acc%d" % which, name="acc%d" % which)
+                if k == NGR - 1:
+                    acc = psx.tile([P, 512], F32, tag="xt", name="acc_last")
+                else:
+                    acc = psa.tile([P, 512], F32, tag="acc%d" % which, name="acc%d" % which)
                 for i in GROUPS[k]:
                     codes, scl = state[("q", i, which)]
                     w = P * SIZES[i]
@@ -152,7 +155,11 @@ def tile_ternarylinear_t_kernel(tc, x, weight_logits, scale, shift, noise, out):
                 state[("a", k, which)] = acc
 
         def noise_transposes(k):
-            nt = psa.tile([P, 512], BF16, tag="nt", name="nt")
+            if k < NGR - 2:
+                nt = psa.tile([P, 512], BF16, tag="nt", name="nt")[:]
+            else:
+                nt_bank = psx.tile([P, 512], F32, tag="xt", name="nt_bank")
+                nt = nt_bank[:].bitcast(BF16)
             for j in range(tiles(k)):
                 col = N_OUT * (first(k) + j)
                 nc.tensor.transpose(nt[:, P * j : P * (j + 1)], noise_sb[:, col : col + N_OUT], ident_b[:])
@@ -178,7 +185,7 @@ def tile_ternarylinear_t_kernel(tc, x, weight_logits, scale, shift, noise, out):
             state[("t", k)] = tt
 
         def join(k):
-            zt = psa.tile([P, 512], F32, tag="zt", name="zt")
+            zt = psa.tile([P, 512], F32, tag={NGR - 2: "acc1", NGR - 1: "acc0"}.get(k, "zt"), name="zt")
             for j in range(tiles(k)):
                 sl = slice(P * j, P * (j + 1))
                 nc.tensor.matmul(out=zt[:, sl], lhsT=state[("m", k)][:, sl], rhs=ident_f[:], is_transpose=True, start=True, stop=False)
@@ -226,14 +233,18 @@ def tile_ternarylinear_t_kernel(tc, x, weight_logits, scale, shift, noise, out):
         per_out = const.tile([P, 2], F32)
 
         def weight_sigmoids():
-            nc.scalar.activation(out=p_mag[:], in_=lv[:, 0], func=ACT.Sigmoid)
-            nc.scalar.activation(out=sgn[:], in_=lv[:, 1], func=ACT.Tanh, scale=0.5)
+            for e in range(2):
+                nc.scalar.activation(out=p_mag[:, e], in_=lv[:, 0, e], func=ACT.Sigmoid)
+                nc.scalar.activation(out=sgn[:, e], in_=lv[:, 1, e], func=ACT.Tanh, scale=0.5)
             nc.scalar.activation(out=warm[:, 1:2], in_=warm[:, 0:1], func=ACT.Sqrt)
 
         def weight_values():
-            nc.vector.tensor_tensor(out=wm32[:], in0=p_mag[:], in1=sgn[:], op=ALU.mult)
-            nc.vector.tensor_tensor(out=wm_sq[:], in0=wm32[:], in1=wm32[:], op=ALU.mult)
-            nc.vector.tensor_tensor(out=wv_bf[:], in0=p_mag[:], in1=wm_sq[:], op=ALU.subtract)
+            for e in range(2):
+                nc.vector.tensor_tensor(out=wm32[:, e], in0=p_mag[:, e], in1=sgn[:, e], op=ALU.mult)
+            for e in range(2):
+                nc.vector.tensor_tensor(out=wm_sq[:, e], in0=wm32[:, e], in1=wm32[:, e], op=ALU.mult)
+            for e in range(2):
+                nc.vector.tensor_tensor(out=wv_bf[:, e], in0=p_mag[:, e], in1=wm_sq[:, e], op=ALU.subtract)
 
         def weight_transposes():
             wt = psa.tile([P, 8, P], BF16, tag="acc1", name="wt1")
@@ -290,14 +301,14 @@ def tile_ternarylinear_t_kernel(tc, x, weight_logits, scale, shift, noise, out):
 
         weight_transposes()
 
-        for s in range(1, NGR + 3):
+        for s in range(1, NGR - 1):
             i = s + 2
             if i + 3 < len(SIZES):
                 load(i + 3)
             if s in (2, 6, 10):
                 load_noise((s + 2) // 4)
             if live(s - 1) and s > 1:
-                for which in (0, 1) if live(s + 1) else (1, 0):
+                for which in (0, 1):
                     quantise(i - 1, which)
             if live(s - 2):
                 mx(s - 2)
@@ -326,3 +337,35 @@ def tile_ternarylinear_t_kernel(tc, x, weight_logits, scale, shift, noise, out):
                 noise_term(s - 2)
             if live(s - 3):
                 finish(s - 3)
+
+        last = len(SIZES) - 1
+        quantise(last - 1, 0)
+        quantise(last - 1, 1)
+        mx(NGR - 3)
+        join(NGR - 4)
+        noise_transposes(NGR - 3)
+        new_squares(last)
+        for b in range(SIZES[last]):
+            bank_copy(last, b)
+            if b == 0:
+                square(last, b, "S", 0, S_TOK[last])
+        square_plain(last, 4 * S_TOK[last], 1024 * SIZES[last])
+        noise_transposes(NGR - 2)
+        noise_transposes(NGR - 1)
+        root_and_mean(NGR - 3)
+        finish(NGR - 4)
+        noise_term(NGR - 3)
+        mx(NGR - 2)
+        quantise(last, 1)
+        quantise(last, 0)
+        root_and_mean(NGR - 2)
+        noise_term(NGR - 2)
+        join(NGR - 3)
+        mx(NGR - 1)
+        finish(NGR - 3)
+        root_and_mean(NGR - 1)
+        noise_term(NGR - 1)
+        join(NGR - 2)
+        finish(NGR - 2)
+        join(NGR - 1)
+        finish(NGR - 1)

from contextlib import ExitStack

import concourse.mybir as mybir
from concourse.masks import make_identity

FP8X4 = mybir.dt.float8_e4m3fn_x4
BF16 = mybir.dt.bfloat16
F32 = mybir.dt.float32
U32 = mybir.dt.uint32
U8 = mybir.dt.uint8
ACT = mybir.ActivationFunctionType
ALU = mybir.AluOpType

N_TOK, K_IN, N_OUT = 8192, 1024, 128
FLOPS = 2 * 2 * N_TOK * K_IN * N_OUT
P = 128
T = N_TOK // P
SIZES = [1, 1, 2] + [4] * 14 + [2, 2]
STARTS = [sum(SIZES[:i]) for i in range(len(SIZES))]
GROUPS = [[0, 1, 2]] + [[i] for i in range(3, len(SIZES))]
NGR = len(GROUPS)
S_TOK = [0,0,0]+[208]*12+[256]*2+[256,256]


def tile_ternarylinear_t_kernel(tc, x, weight_logits, scale, shift, noise, out):
    nc = tc.nc

    with ExitStack() as ctx:
        ctx.enter_context(tc.manual_schedule())
        const = ctx.enter_context(tc.tile_pool(name="const", bufs=1))
        xpool = ctx.enter_context(tc.tile_pool(name="xpool", bufs=6))
        gxpool = ctx.enter_context(tc.tile_pool(name="gxpool", bufs=3))
        gspool = ctx.enter_context(tc.tile_pool(name="gspool", bufs=2))
        cpool = ctx.enter_context(tc.tile_pool(name="cpool", bufs=4))
        epool = ctx.enter_context(tc.tile_pool(name="epool", bufs=3))
        psx = ctx.enter_context(tc.psum_pool(name="psx", bufs=4))
        psa = ctx.enter_context(tc.psum_pool(name="psa", bufs=1))

        state = {}

        def tiles(k):
            return sum(SIZES[i] for i in GROUPS[k])

        def first(k):
            return STARTS[GROUPS[k][0]]

        def group_rows(a, k):
            return a[P * first(k) : P * (first(k) + tiles(k)), :].rearrange("(p j) c -> p (j c)", j=tiles(k))

        def load(i):
            n, t0 = SIZES[i], STARTS[i]
            xt = xpool.tile([P, 4 * K_IN], BF16, tag="x", name="xt")
            k = [g for g in range(NGR) if i in GROUPS[g]][0]
            j = t0 - first(k)
            rows_v = group_rows(x, k)
            nc.sync.dma_start(out=xt[:, : n * K_IN], in_=rows_v[:, K_IN * j : K_IN * (j + n)])
            state[("x", i)] = xt

        def load_noise(q):
            for k in range(NGR):
                if first(k) // (T // 4) == q:
                    lo = N_OUT * first(k)
                    nc.sync.dma_start(out=noise_sb[:, lo : lo + N_OUT * tiles(k)], in_=group_rows(noise, k))

        def x_transposes(i, b):
            n = SIZES[i]
            xw = state[("x", i)][:].bitcast(F32)
            bank = psx.tile([P, 512], F32, tag="xt", name="bank")
            for q in range(4):
                if n == 1:
                    col = P * q
                else:
                    g, h = divmod(b, n // 2)
                    u, j2 = divmod(q, 2)
                    col = 512 * (2 * h + j2) + 256 * g + 128 * u
                nc.tensor.transpose(bank[:, P * q : P * (q + 1)], xw[:, col : col + P], ident_f[:])
            state[("b", i, b)] = bank

        def bank_copy(i, b):
            if b == 0:
                state[("gx", i)] = gxpool.tile([P, 4096], BF16, tag="gx", name="gx", align_bytes=64)
            gx = state[("gx", i)]
            bank = state[("b", i, b)]
            words = gx[:].bitcast(F32)[:, 512 * b : 512 * (b + 1)]
            if SIZES[i] == 1:
                nc.scalar.copy(
                    out=words.rearrange("p (g t u) -> p g t u", g=2, u=2), in_=bank[:].rearrange("p (g u t) -> p g t u", g=2, u=2)
                )
            else:
                nc.scalar.copy(out=words.rearrange("p (t u) -> p t u", u=2), in_=bank[:].rearrange("p (u t) -> p t u", u=2))

        def first_copy():
            gx = gxpool.tile([P, 4096], BF16, tag="gx", name="gx", align_bytes=64)
            state[("gx", 0)] = gx
            nc.vector.tensor_copy(
                out=gx[:].bitcast(F32)[:, :512].rearrange("p (g t u) -> p g t u", g=2, u=2),
                in_=state[("b", 0, 0)][:].rearrange("p (g u t) -> p g t u", g=2, u=2),
            )

        def new_squares(i):
            state[("gs", i)] = gspool.tile([P, 4096], BF16, tag="gs", name="gs", align_bytes=64)

        def square_plain(i, lo, hi):
            gx, gs = state[("gx", i)], state[("gs", i)]
            nc.vector.tensor_tensor(out=gs[:, lo:hi], in0=gx[:, lo:hi], in1=gx[:, lo:hi], op=ALU.mult)

        def square(i, b, who, lo, hi):
            gx, gs = state[("gx", i)], state[("gs", i)]
            a, z = 1024 * b + 4 * lo, 1024 * b + 4 * hi
            quads = state[("b", i, b)][:].bitcast(BF16).rearrange("p (u t e) -> p t u e", u=2, e=2)[:, lo:hi]
            if who == "G":
                nc.gpsimd.tensor_tensor(out=gs[:, a:z], in0=gx[:, a:z], in1=gx[:, a:z], op=ALU.mult)
            elif who == "W":
                nc.vector.tensor_tensor(out=gs[:, a:z], in0=gx[:, a:z], in1=gx[:, a:z], op=ALU.mult)
            elif who == "V":
                nc.vector.tensor_tensor(
                    out=gs[:, a:z].rearrange("p (t u e) -> p t u e", u=2, e=2),
                    in0=quads,
                    in1=gx[:, a:z].rearrange("p (t u e) -> p t u e", u=2, e=2),
                    op=ALU.mult,
                )
            else:
                nc.scalar.activation(out=gs[:, a:z].rearrange("p (t u e) -> p t u e", u=2, e=2), in_=quads, func=ACT.Square)

        def quantise(i, which):
            src = state[(("gx", "gs")[which], i)]
            n = SIZES[i]
            nm = "xs"[which]
            codes = cpool.tile([P, 1024], U32, tag="c" + nm, name="codes_" + nm, align_bytes=64)
            scl = cpool.tile([P, 1024], U8, tag="p" + nm, name="scl_" + nm, align_bytes=64)
            nc.vector.quantize_mx(out=codes[:, : 256 * n].bitcast(FP8X4), scales=scl[:, : 256 * n], in_=src[:, : 1024 * n])
            state[("q", i, which)] = (codes, scl)

        def mx(k):
            for which in (1, 0):
                if k == NGR - 1:
                    acc = psx.tile([P, 512], F32, tag="xt", name="acc_last")
                else:
                    acc = psa.tile([P, 512], F32, tag="acc%d" % which, name="acc%d" % which)
                for i in GROUPS[k]:
                    codes, scl = state[("q", i, which)]
                    w = P * SIZES[i]
                    o = P * (STARTS[i] - first(k))
                    for g in range(2):
                        w0 = P * (2 * which + g)
                        nc.tensor.matmul_mx(
                            out=acc[:, o : o + w],
                            lhsT=w_codes[:, w0 : w0 + P].bitcast(FP8X4),
                            lhsT_scale=w_scales[:, w0 : w0 + P],
                            rhs=codes[:, w * g : w * (g + 1)].bitcast(FP8X4),
                            rhs_scale=scl[:, w * g : w * (g + 1)],
                            start=(g == 0),
                            stop=(g == 1),
                        )
                state[("a", k, which)] = acc

        def noise_transposes(k):
            if k < NGR - 2:
                nt = psa.tile([P, 512], BF16, tag="nt", name="nt")[:]
            else:
                nt_bank = psx.tile([P, 512], F32, tag="xt", name="nt_bank")
                nt = nt_bank[:].bitcast(BF16)
            for j in range(tiles(k)):
                col = N_OUT * (first(k) + j)
                nc.tensor.transpose(nt[:, P * j : P * (j + 1)], noise_sb[:, col : col + N_OUT], ident_b[:])
            state[("n", k)] = nt

        def root_and_mean(k):
            w = P * tiles(k)
            sd = epool.tile([P, 512], F32, tag="sd", name="sd")
            nc.scalar.activation(out=sd[:, :w], in_=state[("a", k, 1)][:, :w], func=ACT.Sqrt)
            mm = epool.tile([P, 512], F32, tag="mm", name="mm")
            nc.scalar.activation(
                out=mm[:, :w], in_=state[("a", k, 0)][:, :w], func=ACT.Identity, scale=per_out[:, 0:1], bias=per_out[:, 1:2]
            )
            state[("sd", k)] = sd
            state[("m", k)] = mm

        def noise_term(k):
            w = P * tiles(k)
            tt = epool.tile([P, 512], F32, tag="tt", name="tt")
            nc.vector.scalar_tensor_tensor(
                out=tt[:, :w], in0=state[("sd", k)][:, :w], scalar=per_out[:, 0:1], in1=state[("n", k)][:, :w], op0=ALU.mult, op1=ALU.mult
            )
            state[("t", k)] = tt

        def join(k):
            zt = psa.tile([P, 512], F32, tag={NGR - 2: "acc1", NGR - 1: "acc0"}.get(k, "zt"), name="zt")
            for j in range(tiles(k)):
                sl = slice(P * j, P * (j + 1))
                nc.tensor.matmul(out=zt[:, sl], lhsT=state[("m", k)][:, sl], rhs=ident_f[:], is_transpose=True, start=True, stop=False)
                nc.tensor.matmul(out=zt[:, sl], lhsT=state[("t", k)][:, sl], rhs=ident_f[:], is_transpose=True, start=False, stop=True)
            state[("zt", k)] = zt

        def finish(k):
            w = P * tiles(k)
            ot = epool.tile([P, 512], F32, tag="ot", name="ot")
            nc.scalar.copy(out=ot[:, :w], in_=state[("zt", k)][:, :w])
            nc.sync.dma_start(out=group_rows(out, k), in_=ot[:, :w])

        logit = const.tile([P, 2 * K_IN], BF16)
        noise_sb = const.tile([P, T * N_OUT], BF16)
        rows = const.tile([P, P], BF16)
        nc.gpsimd.memset(rows[:], 0.0)
        load(0)
        nc.scalar.dma_start(out=rows[0:1, :], in_=scale.rearrange("(a o) -> a o", a=1))
        nc.scalar.dma_start(out=rows[1:2, :], in_=shift.rearrange("(a o) -> a o", a=1))
        load(1)
        nc.sync.dma_start(out=logit[:], in_=weight_logits.rearrange("o i c -> o (i c)"))
        load(2)
        load(3)
        load_noise(0)
        load(4)
        load(5)

        warm = const.tile([P, 3], F32)
        nc.gpsimd.memset(warm[:], 1.0)
        ident_f = const.tile([P, P], F32)
        make_identity(nc, ident_f[:])
        ident_b = const.tile([P, P], BF16)
        make_identity(nc, ident_b[:])
        nc.scalar.activation(out=warm[:, 2:3], in_=warm[:, 0:1], func=ACT.Sigmoid)

        lv = logit[:].rearrange("o (j e c) -> o c e j", e=2, c=2)
        p_mag = const.tile([P, 2, 512], F32)
        sgn = const.tile([P, 2, 512], F32)
        wm32 = const.tile([P, 2, 512], F32)
        wm_sq = const.tile([P, 2, 512], F32)
        wv_bf = const.tile([P, 2, 512], BF16)
        w_grp = const.tile([P, 2, 2, N_OUT, 4], BF16, align_bytes=64)
        w_codes = const.tile([P, 4 * N_OUT], U32, align_bytes=64)
        w_scales = const.tile([P, 4 * N_OUT], U8, align_bytes=64)
        per_out = const.tile([P, 2], F32)

        def weight_sigmoids():
            for e in range(2):
                nc.scalar.activation(out=p_mag[:, e], in_=lv[:, 0, e], func=ACT.Sigmoid)
                nc.scalar.activation(out=sgn[:, e], in_=lv[:, 1, e], func=ACT.Tanh, scale=0.5)
            nc.scalar.activation(out=warm[:, 1:2], in_=warm[:, 0:1], func=ACT.Sqrt)

        def weight_values():
            for e in range(2):
                nc.vector.tensor_tensor(out=wm32[:, e], in0=p_mag[:, e], in1=sgn[:, e], op=ALU.mult)
            for e in range(2):
                nc.vector.tensor_tensor(out=wm_sq[:, e], in0=wm32[:, e], in1=wm32[:, e], op=ALU.mult)
            for e in range(2):
                nc.vector.tensor_tensor(out=wv_bf[:, e], in0=p_mag[:, e], in1=wm_sq[:, e], op=ALU.subtract)

        def weight_transposes():
            wt = psa.tile([P, 8, P], BF16, tag="acc1", name="wt1")
            for m in range(4):
                for e in range(2):
                    nc.tensor.transpose(wt[:, 2 * m + e, :], wv_bf[:, e, P * m : P * (m + 1)], ident_b[:])
            state[("wt", 1)] = wt
            for g, tag in enumerate(("acc0", "zt")):
                wt = psa.tile([P, 4, P], F32, tag=tag, name="wt0")
                for q in range(4):
                    m, e = divmod(4 * g + q, 2)
                    nc.tensor.transpose(wt[:, q, :], wm32[:, e, P * m : P * (m + 1)], ident_f[:])
                state[("wt", 0, g)] = wt
            rt = psa.tile([P, P], BF16, tag="nt", name="rt")
            nc.tensor.transpose(rt[:], rows[:], ident_b[:])
            state["rt"] = rt

        def weight_copies():
            nc.scalar.copy(out=w_grp[:, 1], in_=state[("wt", 1)][:].rearrange("p (g t) o -> p g o t", t=4))
            for g in range(2):
                nc.scalar.copy(out=w_grp[:, 0, g], in_=state[("wt", 0, g)][:].rearrange("p t o -> p o t"))

        def weight_quantise():
            nc.vector.tensor_copy(out=per_out[:], in_=state["rt"][:, 0:2])
            nc.vector.quantize_mx(
                out=w_codes[:].bitcast(FP8X4),
                scales=w_scales[:],
                in_=w_grp[:].rearrange("p w g o t -> p (w g o t)"),
            )

        def live(k):
            return 0 <= k < NGR

        def small(i):
            new_squares(i)
            square_plain(i, 0, 1024 * SIZES[i])
            quantise(i, 0)
            quantise(i, 1)

        for i in range(3):
            for b in range(SIZES[i]):
                x_transposes(i, b)
        first_copy()
        small(0)
        bank_copy(1, 0)
        small(1)
        weight_sigmoids()
        bank_copy(2, 0)
        bank_copy(2, 1)
        for b in range(4):
            x_transposes(3, b)
        weight_values()
        small(2)

        weight_transposes()

        for s in range(1, NGR - 1):
            i = s + 2
            if i + 3 < len(SIZES):
                load(i + 3)
            if s in (2, 6, 10):
                load_noise((s + 2) // 4)
            if live(s - 1) and s > 1:
                for which in (0, 1):
                    quantise(i - 1, which)
            if live(s - 2):
                mx(s - 2)
            if live(s - 3):
                join(s - 3)
            if live(s - 2):
                noise_transposes(s - 2)
            n = SIZES[i] if live(s) else 0
            if n:
                new_squares(i)
            for b in range(4):
                if b < n:
                    bank_copy(i, b)
                    if b == 0 and S_TOK[i] > 0:
                        square(i, b, "S", 0, S_TOK[i])
                if live(s + 1) and b < SIZES[i + 1]:
                    x_transposes(i + 1, b)
                if s == 1 and b == 3:
                    weight_copies()
            if n:
                square_plain(i, 4 * S_TOK[i], 1024 * n)
            if s == 1:
                weight_quantise()
            if live(s - 2):
                root_and_mean(s - 2)
                noise_term(s - 2)
            if live(s - 3):
                finish(s - 3)

        last = len(SIZES) - 1
        quantise(last - 1, 0)
        quantise(last - 1, 1)
        mx(NGR - 3)
        join(NGR - 4)
        noise_transposes(NGR - 3)
        new_squares(last)
        for b in range(SIZES[last]):
            bank_copy(last, b)
            if b == 0:
                square(last, b, "S", 0, S_TOK[last])
        square_plain(last, 4 * S_TOK[last], 1024 * SIZES[last])
        noise_transposes(NGR - 2)
        noise_transposes(NGR - 1)
        root_and_mean(NGR - 3)
        finish(NGR - 4)
        noise_term(NGR - 3)
        mx(NGR - 2)
        quantise(last, 1)
        quantise(last, 0)
        root_and_mean(NGR - 2)
        noise_term(NGR - 2)
        join(NGR - 3)
        mx(NGR - 1)
        finish(NGR - 3)
        root_and_mean(NGR - 1)
        noise_term(NGR - 1)
        join(NGR - 2)
        finish(NGR - 2)
        join(NGR - 1)
        finish(NGR - 1)
